import numpy as np
import ml_dtypes


def mxq(x, axis, fmt="e4m3"):
    dtype, down = {"e4m3": (ml_dtypes.float8_e4m3fn, 7), "e5m2": (ml_dtypes.float8_e5m2, 14)}[fmt]
    v = np.moveaxis(np.asarray(x, np.float32).astype(ml_dtypes.bfloat16).astype(np.float64), axis, -1)
    blocks = v.reshape(v.shape[:-1] + (-1, 32))
    amax = np.abs(blocks).max(-1, keepdims=True)
    byte = np.maximum(np.where(amax > 0, np.frexp(amax)[1] - 1 + 127, 0) - down, 1)
    scale = np.exp2(byte - 127.0)
    codes = (blocks / scale).astype(np.float32).astype(dtype).astype(np.float64)
    return np.moveaxis((codes * scale).reshape(v.shape), -1, axis)


WIDE = False


def mx_kscale(k):
    if not WIDE:
        return np.ones(k)
    levels = np.array([10, -10, 5, -5, 0])
    a = np.random.permutation(np.resize(levels, k // 512 * 4)).reshape(k // 512, 4)
    idx = np.arange(k)
    return np.exp2(a[idx // 512, idx % 128 // 32])


BF16 = ml_dtypes.bfloat16


def bf(x):
    return np.asarray(x, np.float32).astype(BF16)


def f64(x):
    return np.asarray(x).astype(np.float64)


L, B, D, F, TC = 8, 4096, 512, 1024, 4
EPS = 1e-5
NT = 100
ERF_C = 1.0 / np.cumprod(2.0 * np.arange(NT) + 1.0)


def erf(v):
    a = np.minimum(np.abs(v), 6.0)
    q = 2.0 * a * a
    acc = np.full_like(q, ERF_C[-1])
    for c in ERF_C[-2::-1]:
        acc = acc * q + c
    return np.sign(v) * (2.0 / np.sqrt(np.pi)) * a * np.exp(-a * a) * acc


def gelu(v):
    return 0.5 * v * (1.0 + erf(v / np.sqrt(2.0)))


def layer_norm(x, g, b):
    m = x.mean(-1, keepdims=True)
    v = ((x - m) ** 2).mean(-1, keepdims=True)
    return (x - m) / np.sqrt(v + EPS) * g + b


def setup_inputs():
    s, t = mx_kscale(D), mx_kscale(F)
    return {"z": bf(np.random.standard_normal((B, D)) * s),
            "W1": bf(np.random.standard_normal((D, F)) / np.sqrt(D) / s[:, None]),
            "b1": bf(np.random.standard_normal(F) * 0.3),
            "g1": bf((1.0 + 0.1 * np.random.standard_normal(F)) * t),
            "be1": bf(0.1 * np.random.standard_normal(F) * t),
            "W2": bf(np.random.standard_normal((F, D)) / np.sqrt(F) / t[:, None]),
            "b2": bf(np.random.standard_normal(D) * 0.3),
            "g2": bf(1.0 + 0.1 * np.random.standard_normal(D)),
            "be2": bf(0.1 * np.random.standard_normal(D))}


def reference(z, W1, b1, g1, be1, W2, b2, g2, be2):
    h = gelu((mxq(f64(z), 1, "e4m3") @ mxq(f64(W1), 0, "e4m3")) + f64(b1))
    h = layer_norm(h, f64(g1), f64(be1))
    return layer_norm((mxq(h, 1, "e4m3") @ mxq(f64(W2), 0, "e4m3")) + f64(b2), f64(g2), f64(be2))

@@ -1,0 +1,252 @@
+from contextlib import ExitStack
+
+import concourse.mybir as mybir
+from concourse.masks import make_identity
+
+F32 = mybir.dt.float32
+BF16 = mybir.dt.bfloat16
+U32 = mybir.dt.uint32
+U8 = mybir.dt.uint8
+FP8X4 = mybir.dt.float8_e4m3fn_x4
+ACT = mybir.ActivationFunctionType
+ALU = mybir.AluOpType
+
+P = 128
+B, D, F = 4096, 512, 1024
+EPS = 1e-5
+TB = 4
+BLK = TB * P
+NBLK = B // BLK
+FLOPS = 2 * B * D * F * 2
+
+
+def regroup(nc, dst, src):
+    nc.vector.tensor_copy(
+        out=dst.rearrange("p (c i) t -> p c t i", i=4),
+        in_=src.rearrange("p t (c i) -> p c t i", i=4),
+    )
+
+
+def tile_emaaggregator_pa_t_kernel(tc, z, W1, b1, g1, be1, W2, b2, g2, be2, out):
+    nc = tc.nc
+    with ExitStack() as ctx:
+        const = ctx.enter_context(tc.tile_pool(name="const", bufs=1))
+        wst = ctx.enter_context(tc.tile_pool(name="wst", bufs=1))
+        zin = ctx.enter_context(tc.tile_pool(name="zin", bufs=4))
+        zq = ctx.enter_context(tc.tile_pool(name="zq", bufs=2))
+        xp = ctx.enter_context(tc.tile_pool(name="xp", bufs=3))
+        gp = ctx.enter_context(tc.tile_pool(name="gp", bufs=10))
+        jp = ctx.enter_context(tc.tile_pool(name="jp", bufs=2))
+        hp = ctx.enter_context(tc.tile_pool(name="hp", bufs=2))
+        op = ctx.enter_context(tc.tile_pool(name="op", bufs=3))
+        ob = ctx.enter_context(tc.tile_pool(name="ob", bufs=2))
+        sm = ctx.enter_context(tc.tile_pool(name="sm", bufs=8))
+        ps = ctx.enter_context(tc.psum_pool(name="ps", bufs=2))
+
+        w1r = wst.tile([P, 4, F], BF16, tag="wr", bufs=2)
+        for u in range(2):
+            nc.sync.dma_start(
+                out=w1r[:, 2 * u : 2 * u + 2, :],
+                in_=W1[256 * u : 256 * (u + 1), :].rearrange("(q e) c -> q e c", e=2),
+            )
+        z_sb = []
+
+        def load_z(b):
+            zt_in = zin.tile([P, TB * D], BF16, tag="z")
+            nc.sync.dma_start(
+                out=zt_in[:],
+                in_=z[BLK * b : BLK * (b + 1), :].rearrange("(p j) k -> p (j k)", j=TB),
+            )
+            z_sb.append(zt_in)
+
+        load_z(0)
+        b1b = const.tile([P, F], BF16)
+        nc.sync.dma_start(out=b1b[:], in_=b1.partition_broadcast(P))
+        load_z(1)
+        w2r = wst.tile([P, 8, D], BF16, tag="wr", bufs=2)
+        nc.sync.dma_start(out=w2r[:], in_=W2.rearrange("(ct p) n -> p ct n", p=P))
+        b2b = const.tile([P, D], BF16)
+        nc.sync.dma_start(out=b2b[:], in_=b2.partition_broadcast(P))
+        g2b = const.tile([P, D], BF16)
+        nc.sync.dma_start(out=g2b[:], in_=g2.partition_broadcast(P))
+        be2b = const.tile([P, D], BF16)
+        nc.sync.dma_start(out=be2b[:], in_=be2.partition_broadcast(P))
+
+        ident = const.tile([P, P], F32)
+        make_identity(nc, ident[:])
+        neg_half = const.tile([P, 1], F32)
+        nc.vector.memset(neg_half[:], -0.5)
+        warm = const.tile([P, 1], F32)
+        nc.vector.memset(warm[:], 0.0)
+        warm2 = const.tile([P, 1], F32)
+        nc.scalar.activation(out=warm2[:], in_=warm[:], func=ACT.Gelu)
+
+        gb_rows = const.tile([P, P], BF16)
+        nc.vector.memset(gb_rows[:], 0.0)
+        nc.scalar.dma_start(out=gb_rows[0:8, :], in_=g1.rearrange("(r c) -> r c", c=P))
+        nc.scalar.dma_start(out=gb_rows[8:16, :], in_=be1.rearrange("(r c) -> r c", c=P))
+        gb_f = const.tile([P, P], F32)
+        nc.vector.tensor_copy(out=gb_f[:], in_=gb_rows[:])
+        gb_ps = ps.tile([P, P], F32, tag="zt", bufs=1)
+        nc.tensor.transpose(gb_ps[:], gb_f[:], ident[:])
+        gb_col = const.tile([P, 16], F32)
+        nc.vector.tensor_copy(out=gb_col[:], in_=gb_ps[:, 0:16])
+
+        w1g = wst.tile([P, F, 4], BF16, tag="wg", align_bytes=64)
+        w1c = const.tile([P, F], U32, align_bytes=64)
+        w1s = const.tile([P, F], U8, align_bytes=64)
+        for h in range(2):
+            cols = slice(512 * h, 512 * (h + 1))
+            regroup(nc, w1g[:, cols, :], w1r[:, :, cols])
+        for h in range(2):
+            cols = slice(512 * h, 512 * (h + 1))
+            nc.vector.quantize_mx(
+                out=w1c[:, cols].bitcast(FP8X4),
+                scales=w1s[:, cols],
+                in_=w1g[:, cols, :].rearrange("p w t -> p (w t)"),
+            )
+        w2c = const.tile([P, 2, D], U32, align_bytes=64)
+        w2s = const.tile([P, 2, D], U8, align_bytes=64)
+
+        def prep_w2():
+            w2g = wst.tile([P, 2, D, 4], BF16, tag="wg", align_bytes=64)
+            for c in range(2):
+                regroup(nc, w2g[:, c], w2r[:, 4 * c : 4 * c + 4, :])
+            for c in range(2):
+                nc.vector.quantize_mx(
+                    out=w2c[:, c, :].bitcast(FP8X4),
+                    scales=w2s[:, c, :],
+                    in_=w2g[:, c].rearrange("p w t -> p (w t)"),
+                )
+
+        def stage_z(b):
+            zw = z_sb[b][:].bitcast(F32)
+            zg = zq.tile([P, TB * P * 2], F32, tag="zg", align_bytes=64)
+            zgv = zg[:].rearrange("q (j t u) -> q j t u", j=TB, u=2)
+            for half in range(2):
+                zt = ps.tile([P, 2, 2, P], F32, tag="zt", bufs=1)
+                for jj in range(2):
+                    j = 2 * half + jj
+                    for u in range(2):
+                        c0 = j * 256 + u * P
+                        nc.tensor.transpose(zt[:, jj, u, :], zw[:, c0 : c0 + P], ident[:])
+                nc.scalar.copy(
+                    out=zgv[:, 2 * half : 2 * half + 2, :, :],
+                    in_=zt[:].rearrange("q j u t -> q j t u"),
+                )
+            zc = zq.tile([P, BLK], U32, tag="zc", align_bytes=64)
+            zs = zq.tile([P, BLK], U8, tag="zs", align_bytes=64)
+            nc.vector.quantize_mx(out=zc[:].bitcast(FP8X4), scales=zs[:], in_=zg[:].bitcast(BF16))
+            return zc, zs
+
+        def rstd_of(ss, inv_n, tag):
+            ve = sm.tile([P, 1], F32, tag=tag + "ve")
+            nc.gpsimd.tensor_scalar(out=ve[:], in0=ss[:], scalar1=inv_n, scalar2=EPS, op0=ALU.mult, op1=ALU.add)
+            rstd = sm.tile([P, 1], F32, tag=tag + "rs")
+            nc.gpsimd.tensor_tensor(out=rstd[:], in0=ve[:], in1=neg_half[:], op=ALU.pow)
+            return rstd
+
+        def stage_hidden(zc, zs):
+            n_tiles = []
+            for j in range(TB):
+                tok = slice(P * j, P * (j + 1))
+                x = xp.tile([P, F], F32, tag="x")
+                for h in range(2):
+                    cols = slice(512 * h, 512 * (h + 1))
+                    acc = ps.tile([P, 512], F32, tag="mm1", bufs=3)
+                    nc.tensor.matmul_mx(
+                        out=acc[:],
+                        lhsT=zc[:, tok].bitcast(FP8X4),
+                        lhsT_scale=zs[:, tok],
+                        rhs=w1c[:, cols].bitcast(FP8X4),
+                        rhs_scale=w1s[:, cols],
+                        start=True,
+                        stop=True,
+                    )
+                    nc.vector.tensor_tensor(out=x[:, cols], in0=acc[:], in1=b1b[:, cols], op=ALU.add)
+                g = gp.tile([P, F], F32, tag="g")
+                s1 = sm.tile([P, 1], F32, tag="s1")
+                nc.scalar.activation(out=g[:], in_=x[:], func=ACT.Gelu, accum_out=s1[:])
+                nm = sm.tile([P, 1], F32, tag="nm")
+                nc.gpsimd.tensor_scalar(out=nm[:], in0=s1[:], scalar1=-1.0 / F, scalar2=0.0, op0=ALU.mult, op1=ALU.add)
+                junk = jp.tile([P, F], BF16, tag="junk")
+                ss = sm.tile([P, 1], F32, tag="ss")
+                nc.scalar.activation(out=junk[:], in_=g[:], func=ACT.Square, bias=nm[:], accum_out=ss[:])
+                rstd = rstd_of(ss, 1.0 / F, "a")
+                nc.vector.tensor_scalar(out=g[:], in0=g[:], scalar1=nm[:], scalar2=rstd[:], op0=ALU.add, op1=ALU.mult)
+                n_tiles.append(g)
+            return n_tiles
+
+        def stage_hq(n_tiles):
+            hb = hp.tile([P, 8, BLK], BF16, tag="hb")
+            for ct in range(8):
+                ht = ps.tile([P, BLK], F32, tag="ht", bufs=2)
+                for j in range(TB):
+                    nc.tensor.transpose(ht[:, P * j : P * (j + 1)], n_tiles[j][:, P * ct : P * (ct + 1)], ident[:])
+                nc.scalar.activation(
+                    out=hb[:, ct, :],
+                    in_=ht[:],
+                    func=ACT.Identity,
+                    scale=gb_col[:, ct : ct + 1],
+                    bias=gb_col[:, 8 + ct : 9 + ct],
+                )
+            hg = hp.tile([P, 2, BLK, 4], BF16, tag="hg", align_bytes=64)
+            hc = hp.tile([P, 2, BLK], U32, tag="hc", align_bytes=64)
+            hs = hp.tile([P, 2, BLK], U8, tag="hs", align_bytes=64)
+            for c in range(2):
+                regroup(nc, hg[:, c], hb[:, 4 * c : 4 * c + 4, :])
+            for c in range(2):
+                nc.vector.quantize_mx(
+                    out=hc[:, c, :].bitcast(FP8X4),
+                    scales=hs[:, c, :],
+                    in_=hg[:, c].rearrange("p w t -> p (w t)"),
+                )
+            return hc, hs
+
+        def stage_out(b, hc, hs):
+            o = ob.tile([P, TB, D], F32, tag="o")
+            for j in range(TB):
+                tok = slice(P * j, P * (j + 1))
+                y = ps.tile([P, D], F32, tag="y", bufs=2)
+                for c in range(2):
+                    nc.tensor.matmul_mx(
+                        out=y[:],
+                        lhsT=hc[:, c, tok].bitcast(FP8X4),
+                        lhsT_scale=hs[:, c, tok],
+                        rhs=w2c[:, c, :].bitcast(FP8X4),
+                        rhs_scale=w2s[:, c, :],
+                        start=(c == 0),
+                        stop=(c == 1),
+                    )
+                x2 = op.tile([P, D], F32, tag="x2")
+                s2 = sm.tile([P, 1], F32, tag="s2")
+                nc.vector.scalar_tensor_tensor(
+                    out=x2[:], in0=y[:], scalar=1.0, in1=b2b[:], op0=ALU.mult, op1=ALU.add, accum_out=s2[:]
+                )
+                nm2 = sm.tile([P, 1], F32, tag="nm2")
+                nc.gpsimd.tensor_scalar(out=nm2[:], in0=s2[:], scalar1=-1.0 / D, scalar2=0.0, op0=ALU.mult, op1=ALU.add)
+                junk2 = jp.tile([P, D], BF16, tag="junk2")
+                ss2 = sm.tile([P, 1], F32, tag="ss2")
+                nc.scalar.activation(out=junk2[:], in_=x2[:], func=ACT.Square, bias=nm2[:], accum_out=ss2[:])
+                rstd2 = rstd_of(ss2, 1.0 / D, "b")
+                t2 = op.tile([P, D], F32, tag="t2")
+                nc.vector.scalar_tensor_tensor(
+                    out=t2[:], in0=x2[:], scalar=nm2[:], in1=g2b[:], op0=ALU.add, op1=ALU.mult
+                )
+                nc.vector.scalar_tensor_tensor(
+                    out=o[:, j, :], in0=t2[:], scalar=rstd2[:], in1=be2b[:], op0=ALU.mult, op1=ALU.add
+                )
+            nc.sync.dma_start(
+                out=out[BLK * b : BLK * (b + 1), :].rearrange("(p j) d -> p (j d)", j=TB),
+                in_=o[:].rearrange("p j d -> p (j d)"),
+            )
+
+        for b in range(NBLK):
+            if b + 2 < NBLK:
+                load_z(b + 2)
+            zc, zs = stage_z(b)
+            n_tiles = stage_hidden(zc, zs)
+            if b == 0:
+                prep_w2()
+            hc, hs = stage_hq(n_tiles)
+            stage_out(b, hc, hs)

@@ -14,10 +14,10 @@ ALU = mybir.AluOpType
 P = 128
 B, D, F = 4096, 512, 1024
 EPS = 1e-5
-TB = 4
-BLK = TB * P
-NBLK = B // BLK
+NT = [4, 4, 4, 4, 4, 4, 4, 4]
 FLOPS = 2 * B * D * F * 2
+NORM_ON_G = False
+A_ON_V = ((0, 1), (0, 3), (0, 5), (0, 7))
 
 
 def regroup(nc, dst, src):
@@ -29,41 +29,51 @@ def regroup(nc, dst, src):
 
 def tile_emaaggregator_pa_t_kernel(tc, z, W1, b1, g1, be1, W2, b2, g2, be2, out):
     nc = tc.nc
+    nb = len(NT)
+    tok0 = [P * sum(NT[:b]) for b in range(nb)]
     with ExitStack() as ctx:
         const = ctx.enter_context(tc.tile_pool(name="const", bufs=1))
         wst = ctx.enter_context(tc.tile_pool(name="wst", bufs=1))
         zin = ctx.enter_context(tc.tile_pool(name="zin", bufs=4))
-        zq = ctx.enter_context(tc.tile_pool(name="zq", bufs=2))
-        xp = ctx.enter_context(tc.tile_pool(name="xp", bufs=3))
-        gp = ctx.enter_context(tc.tile_pool(name="gp", bufs=10))
+        zq_pool = ctx.enter_context(tc.tile_pool(name="zq", bufs=2))
+        xp = ctx.enter_context(tc.tile_pool(name="xp", bufs=4))
+        gp = ctx.enter_context(tc.tile_pool(name="gp", bufs=8))
         jp = ctx.enter_context(tc.tile_pool(name="jp", bufs=2))
         hp = ctx.enter_context(tc.tile_pool(name="hp", bufs=2))
-        op = ctx.enter_context(tc.tile_pool(name="op", bufs=3))
+        op = ctx.enter_context(tc.tile_pool(name="op", bufs=5))
         ob = ctx.enter_context(tc.tile_pool(name="ob", bufs=2))
-        sm = ctx.enter_context(tc.tile_pool(name="sm", bufs=8))
-        ps = ctx.enter_context(tc.psum_pool(name="ps", bufs=2))
-
-        w1r = wst.tile([P, 4, F], BF16, tag="wr", bufs=2)
-        for u in range(2):
-            nc.sync.dma_start(
-                out=w1r[:, 2 * u : 2 * u + 2, :],
-                in_=W1[256 * u : 256 * (u + 1), :].rearrange("(q e) c -> q e c", e=2),
-            )
-        z_sb = []
+        sm = ctx.enter_context(tc.tile_pool(name="sm", bufs=12))
+        ps = ctx.enter_context(tc.psum_pool(name="ps", bufs=4))
+        ctx.enter_context(tc.manual_schedule())
+        st = [dict() for b in range(nb)]
 
         def load_z(b):
-            zt_in = zin.tile([P, TB * D], BF16, tag="z")
+            nt = NT[b]
+            z_sb = zin.tile([P, nt * D], BF16, tag="z")
             nc.sync.dma_start(
-                out=zt_in[:],
-                in_=z[BLK * b : BLK * (b + 1), :].rearrange("(p j) k -> p (j k)", j=TB),
+                out=z_sb[:],
+                in_=z[tok0[b] : tok0[b] + nt * P, :].rearrange("(p j) k -> p (j k)", j=nt),
             )
-            z_sb.append(zt_in)
+            st[b]["z"] = z_sb
 
         load_z(0)
+        w1r0 = wst.tile([P, 4, 512], BF16)
+        w1r1 = wst.tile([P, 4, 512], BF16)
+        w1r = [w1r0, w1r1]
+        for h in range(2):
+            for u in range(2):
+                nc.sync.dma_start(
+                    out=w1r[h][:, 2 * u : 2 * u + 2, :],
+                    in_=W1[256 * u : 256 * (u + 1), 512 * h : 512 * (h + 1)].rearrange("(q e) c -> q e c", e=2),
+                )
+        gb_rows = const.tile([P, P], BF16)
+        nc.vector.memset(gb_rows[:], 0.0)
+        nc.scalar.dma_start(out=gb_rows[0:8, :], in_=g1.rearrange("(r c) -> r c", c=P))
+        nc.scalar.dma_start(out=gb_rows[8:16, :], in_=be1.rearrange("(r c) -> r c", c=P))
         b1b = const.tile([P, F], BF16)
         nc.sync.dma_start(out=b1b[:], in_=b1.partition_broadcast(P))
         load_z(1)
-        w2r = wst.tile([P, 8, D], BF16, tag="wr", bufs=2)
+        w2r = wst.tile([P, 8, D], BF16)
         nc.sync.dma_start(out=w2r[:], in_=W2.rearrange("(ct p) n -> p ct n", p=P))
         b2b = const.tile([P, D], BF16)
         nc.sync.dma_start(out=b2b[:], in_=b2.partition_broadcast(P))
@@ -71,6 +81,7 @@ def tile_emaaggregator_pa_t_kernel(tc, z, W1, b1, g1, be1, W2, b2, g2, be2, out)
         nc.sync.dma_start(out=g2b[:], in_=g2.partition_broadcast(P))
         be2b = const.tile([P, D], BF16)
         nc.sync.dma_start(out=be2b[:], in_=be2.partition_broadcast(P))
+        load_z(2)
 
         ident = const.tile([P, P], F32)
         make_identity(nc, ident[:])
@@ -81,35 +92,208 @@ def tile_emaaggregator_pa_t_kernel(tc, z, W1, b1, g1, be1, W2, b2, g2, be2, out)
         warm2 = const.tile([P, 1], F32)
         nc.scalar.activation(out=warm2[:], in_=warm[:], func=ACT.Gelu)
 
-        gb_rows = const.tile([P, P], BF16)
-        nc.vector.memset(gb_rows[:], 0.0)
-        nc.scalar.dma_start(out=gb_rows[0:8, :], in_=g1.rearrange("(r c) -> r c", c=P))
-        nc.scalar.dma_start(out=gb_rows[8:16, :], in_=be1.rearrange("(r c) -> r c", c=P))
-        gb_f = const.tile([P, P], F32)
-        nc.vector.tensor_copy(out=gb_f[:], in_=gb_rows[:])
-        gb_ps = ps.tile([P, P], F32, tag="zt", bufs=1)
-        nc.tensor.transpose(gb_ps[:], gb_f[:], ident[:])
-        gb_col = const.tile([P, 16], F32)
-        nc.vector.tensor_copy(out=gb_col[:], in_=gb_ps[:, 0:16])
+        def zT(b):
+            nt = NT[b]
+            zw = st[b]["z"][:].bitcast(F32)
+            st[b]["zt"] = []
+            for j0 in range(0, nt, 2):
+                nj = min(2, nt - j0)
+                zt = ps.tile([P, nj, 2, P], F32, tag="Y")
+                for jj in range(nj):
+                    for u in range(2):
+                        c0 = (j0 + jj) * 256 + u * P
+                        nc.tensor.transpose(zt[:, jj, u, :], zw[:, c0 : c0 + P], ident[:])
+                st[b]["zt"].append((j0, nj, zt))
 
-        w1g = wst.tile([P, F, 4], BF16, tag="wg", align_bytes=64)
+        def zo(b):
+            nt = NT[b]
+            zg = zq_pool.tile([P, nt * P * 2], F32, tag="zg", align_bytes=64)
+            zgv = zg[:].rearrange("q (j t u) -> q j t u", j=nt, u=2)
+            for j0, nj, zt in st[b]["zt"]:
+                nc.scalar.copy(out=zgv[:, j0 : j0 + nj, :, :], in_=zt[:].rearrange("q j u t -> q j t u"))
+            st[b]["zg"] = zg
+
+        def zquant(b):
+            nt = NT[b]
+            zc = zq_pool.tile([P, nt * P], U32, tag="zc", align_bytes=64)
+            zs = zq_pool.tile([P, nt * P], U8, tag="zs", align_bytes=64)
+            nc.vector.quantize_mx(out=zc[:].bitcast(FP8X4), scales=zs[:], in_=st[b]["zg"][:].bitcast(BF16))
+            st[b]["zc"], st[b]["zs"] = zc, zs
+            st[b]["x"], st[b]["g"], st[b]["s1"], st[b]["nm"], st[b]["rs"] = {}, {}, {}, {}, {}
+
+        def mm1_bias(b, j):
+            tok = slice(P * j, P * (j + 1))
+            x = xp.tile([P, F], F32, tag="x")
+            for h in range(2):
+                cols = slice(512 * h, 512 * (h + 1))
+                acc = ps.tile([P, 512], F32, tag="X")
+                nc.tensor.matmul_mx(
+                    out=acc[:],
+                    lhsT=st[b]["zc"][:, tok].bitcast(FP8X4),
+                    lhsT_scale=st[b]["zs"][:, tok],
+                    rhs=w1c[:, cols].bitcast(FP8X4),
+                    rhs_scale=w1s[:, cols],
+                    start=True,
+                    stop=True,
+                )
+                nc.vector.tensor_tensor(out=x[:, cols], in0=acc[:], in1=b1b[:, cols], op=ALU.add)
+            st[b]["x"][j] = x
+
+        def gelu(b, j):
+            g = gp.tile([P, F], F32, tag="g")
+            s1 = sm.tile([P, 1], F32, tag="s1")
+            nc.scalar.activation(out=g[:], in_=st[b]["x"][j][:], func=ACT.Gelu, accum_out=s1[:])
+            st[b]["g"][j], st[b]["s1"][j] = g, s1
+
+        def rstd_of(ss, scale, tag):
+            ve = sm.tile([P, 1], F32, tag=tag + "ve")
+            nc.gpsimd.tensor_scalar(out=ve[:], in0=ss[:], scalar1=scale, scalar2=EPS, op0=ALU.mult, op1=ALU.add)
+            rstd = sm.tile([P, 1], F32, tag=tag + "rs")
+            nc.gpsimd.tensor_tensor(out=rstd[:], in0=ve[:], in1=neg_half[:], op=ALU.pow)
+            return rstd
+
+        def squares(b, j):
+            s1 = st[b]["s1"][j]
+            nm = sm.tile([P, 1], F32, tag="nm")
+            nc.gpsimd.tensor_scalar(out=nm[:], in0=s1[:], scalar1=-1.0 / F, scalar2=0.0, op0=ALU.mult, op1=ALU.add)
+            junk = jp.tile([P, F], BF16, tag="junk")
+            ss = sm.tile([P, 1], F32, tag="ss")
+            nc.scalar.activation(out=junk[:], in_=st[b]["g"][j][:], func=ACT.Square, scale=-float(F), bias=s1[:], accum_out=ss[:])
+            st[b]["nm"][j] = nm
+            st[b]["rs"][j] = rstd_of(ss, 1.0 / (float(F) ** 3), "a")
+
+        def norm(b, j):
+            g = st[b]["g"][j]
+            eng = nc.gpsimd if NORM_ON_G else nc.vector
+            eng.tensor_scalar(out=g[:], in0=g[:], scalar1=st[b]["nm"][j][:], scalar2=st[b]["rs"][j][:], op0=ALU.add, op1=ALU.mult)
+
+        def t_affine(b, ct):
+            nt = NT[b]
+            if ct == 0:
+                hb_new = hp.tile([P, 8, nt * P], BF16, tag="hb")
+                st[b]["hb"] = hb_new
+            ht = ps.tile([P, nt * P], F32, tag="X")
+            for j in range(nt):
+                nc.tensor.transpose(ht[:, P * j : P * (j + 1)], st[b]["g"][j][:, P * ct : P * (ct + 1)], ident[:])
+            if (b, ct) in A_ON_V:
+                nc.vector.tensor_scalar(
+                    out=st[b]["hb"][:, ct, :],
+                    in0=ht[:],
+                    scalar1=gb_col[:, ct : ct + 1],
+                    scalar2=gb_col[:, 8 + ct : 9 + ct],
+                    op0=ALU.mult,
+                    op1=ALU.add,
+                )
+            else:
+                nc.scalar.activation(
+                    out=st[b]["hb"][:, ct, :],
+                    in_=ht[:],
+                    func=ACT.Identity,
+                    scale=gb_col[:, ct : ct + 1],
+                    bias=gb_col[:, 8 + ct : 9 + ct],
+                )
+
+        def h_regroup(b, c):
+            nt = NT[b]
+            if c == 0:
+                hg_new = hp.tile([P, 2, nt * P, 4], BF16, tag="hg", align_bytes=64)
+                st[b]["hg"] = hg_new
+            regroup(nc, st[b]["hg"][:, c], st[b]["hb"][:, 4 * c : 4 * c + 4, :])
+
+        def h_quant(b, c):
+            nt = NT[b]
+            if c == 0:
+                hc_new = hp.tile([P, 2, nt * P], U32, tag="hc", align_bytes=64)
+                hs_new = hp.tile([P, 2, nt * P], U8, tag="hs", align_bytes=64)
+                st[b]["hc"], st[b]["hs"] = hc_new, hs_new
+                o_new = ob.tile([P, nt, D], F32, tag="o")
+                st[b]["o"] = o_new
+                st[b]["x2"], st[b]["s2"], st[b]["nm2"], st[b]["rs2"], st[b]["t2"] = {}, {}, {}, {}, {}
+            nc.vector.quantize_mx(
+                out=st[b]["hc"][:, c, :].bitcast(FP8X4),
+                scales=st[b]["hs"][:, c, :],
+                in_=st[b]["hg"][:, c].rearrange("p w t -> p (w t)"),
+            )
+
+        def mm2_bias(b, j):
+            tok = slice(P * j, P * (j + 1))
+            y = ps.tile([P, D], F32, tag="Y")
+            for c in range(2):
+                nc.tensor.matmul_mx(
+                    out=y[:],
+                    lhsT=st[b]["hc"][:, c, tok].bitcast(FP8X4),
+                    lhsT_scale=st[b]["hs"][:, c, tok],
+                    rhs=w2c[:, c, :].bitcast(FP8X4),
+                    rhs_scale=w2s[:, c, :],
+                    start=(c == 0),
+                    stop=(c == 1),
+                )
+            x2 = op.tile([P, D], F32, tag="x2")
+            s2 = sm.tile([P, 1], F32, tag="s2")
+            nc.vector.scalar_tensor_tensor(out=x2[:], in0=y[:], scalar=1.0, in1=b2b[:], op0=ALU.mult, op1=ALU.add, accum_out=s2[:])
+            nm2 = sm.tile([P, 1], F32, tag="nm2")
+            nc.gpsimd.tensor_scalar(out=nm2[:], in0=s2[:], scalar1=-1.0 / D, scalar2=0.0, op0=ALU.mult, op1=ALU.add)
+            st[b]["x2"][j], st[b]["s2"][j], st[b]["nm2"][j] = x2, s2, nm2
+
+        def squares2(b, j):
+            junk2 = jp.tile([P, D], BF16, tag="junk2")
+            ss2 = sm.tile([P, 1], F32, tag="ss2")
+            nc.scalar.activation(out=junk2[:], in_=st[b]["x2"][j][:], func=ACT.Square, scale=-float(D), bias=st[b]["s2"][j][:], accum_out=ss2[:])
+            st[b]["rs2"][j] = rstd_of(ss2, 1.0 / (float(D) ** 3), "b")
+
+        def centre_gain(b, j):
+            t2 = op.tile([P, D], F32, tag="t2")
+            nc.vector.scalar_tensor_tensor(out=t2[:], in0=st[b]["x2"][j][:], scalar=st[b]["nm2"][j][:], in1=g2b[:], op0=ALU.add, op1=ALU.mult)
+            st[b]["t2"][j] = t2
+
+        def scale_shift(b, j):
+            nc.vector.scalar_tensor_tensor(out=st[b]["o"][:, j, :], in0=st[b]["t2"][j][:], scalar=st[b]["rs2"][j][:], in1=be2b[:], op0=ALU.mult, op1=ALU.add)
+
+        def store(b):
+            nt = NT[b]
+            nc.sync.dma_start(
+                out=out[tok0[b] : tok0[b] + nt * P, :].rearrange("(p j) d -> p (j d)", j=nt),
+                in_=st[b]["o"][:].rearrange("p j d -> p (j d)"),
+            )
+
+        def store_tile(b, j):
+            nt = NT[b]
+            nc.sync.dma_start(
+                out=out[tok0[b] : tok0[b] + nt * P, :].rearrange("(p j) d -> p j d", j=nt)[:, j, :],
+                in_=st[b]["o"][:, j, :],
+            )
+
+        zT(0)
+        zo(0)
+        w1g = wst.tile([P, F, 4], BF16, tag="wg", bufs=2, align_bytes=64)
         w1c = const.tile([P, F], U32, align_bytes=64)
         w1s = const.tile([P, F], U8, align_bytes=64)
-        for h in range(2):
-            cols = slice(512 * h, 512 * (h + 1))
-            regroup(nc, w1g[:, cols, :], w1r[:, :, cols])
-        for h in range(2):
+        w2g = wst.tile([P, 2, D, 4], BF16, tag="wg", bufs=2, align_bytes=64)
+        w2c = const.tile([P, 2, D], U32, align_bytes=64)
+        w2s = const.tile([P, 2, D], U8, align_bytes=64)
+        gb_col = const.tile([P, 16], F32)
+
+        def w1_quant(h):
             cols = slice(512 * h, 512 * (h + 1))
             nc.vector.quantize_mx(
                 out=w1c[:, cols].bitcast(FP8X4),
                 scales=w1s[:, cols],
                 in_=w1g[:, cols, :].rearrange("p w t -> p (w t)"),
             )
-        w2c = const.tile([P, 2, D], U32, align_bytes=64)
-        w2s = const.tile([P, 2, D], U8, align_bytes=64)
 
-        def prep_w2():
-            w2g = wst.tile([P, 2, D, 4], BF16, tag="wg", align_bytes=64)
+        regroup(nc, w1g[:, 0:512, :], w1r[0][:])
+        zquant(0)
+        w1_quant(0)
+        regroup(nc, w1g[:, 512:1024, :], w1r[1][:])
+        w1_quant(1)
+
+        def late_setup():
+            zT(1)
+            gb_f = const.tile([P, P], F32)
+            nc.vector.tensor_copy(out=gb_f[:], in_=gb_rows[:])
+            gb_ps = ps.tile([P, P], F32, tag="X")
+            nc.tensor.transpose(gb_ps[:], gb_f[:], ident[:])
+            nc.vector.tensor_copy(out=gb_col[:], in_=gb_ps[:, 0:16])
             for c in range(2):
                 regroup(nc, w2g[:, c], w2r[:, 4 * c : 4 * c + 4, :])
             for c in range(2):
@@ -119,134 +303,55 @@ def tile_emaaggregator_pa_t_kernel(tc, z, W1, b1, g1, be1, W2, b2, g2, be2, out)
                     in_=w2g[:, c].rearrange("p w t -> p (w t)"),
                 )
 
-        def stage_z(b):
-            zw = z_sb[b][:].bitcast(F32)
-            zg = zq.tile([P, TB * P * 2], F32, tag="zg", align_bytes=64)
-            zgv = zg[:].rearrange("q (j t u) -> q j t u", j=TB, u=2)
-            for half in range(2):
-                zt = ps.tile([P, 2, 2, P], F32, tag="zt", bufs=1)
-                for jj in range(2):
-                    j = 2 * half + jj
-                    for u in range(2):
-                        c0 = j * 256 + u * P
-                        nc.tensor.transpose(zt[:, jj, u, :], zw[:, c0 : c0 + P], ident[:])
-                nc.scalar.copy(
-                    out=zgv[:, 2 * half : 2 * half + 2, :, :],
-                    in_=zt[:].rearrange("q j u t -> q j t u"),
-                )
-            zc = zq.tile([P, BLK], U32, tag="zc", align_bytes=64)
-            zs = zq.tile([P, BLK], U8, tag="zs", align_bytes=64)
-            nc.vector.quantize_mx(out=zc[:].bitcast(FP8X4), scales=zs[:], in_=zg[:].bitcast(BF16))
-            return zc, zs
-
-        def rstd_of(ss, inv_n, tag):
-            ve = sm.tile([P, 1], F32, tag=tag + "ve")
-            nc.gpsimd.tensor_scalar(out=ve[:], in0=ss[:], scalar1=inv_n, scalar2=EPS, op0=ALU.mult, op1=ALU.add)
-            rstd = sm.tile([P, 1], F32, tag=tag + "rs")
-            nc.gpsimd.tensor_tensor(out=rstd[:], in0=ve[:], in1=neg_half[:], op=ALU.pow)
-            return rstd
-
-        def stage_hidden(zc, zs):
-            n_tiles = []
-            for j in range(TB):
-                tok = slice(P * j, P * (j + 1))
-                x = xp.tile([P, F], F32, tag="x")
-                for h in range(2):
-                    cols = slice(512 * h, 512 * (h + 1))
-                    acc = ps.tile([P, 512], F32, tag="mm1", bufs=3)
-                    nc.tensor.matmul_mx(
-                        out=acc[:],
-                        lhsT=zc[:, tok].bitcast(FP8X4),
-                        lhsT_scale=zs[:, tok],
-                        rhs=w1c[:, cols].bitcast(FP8X4),
-                        rhs_scale=w1s[:, cols],
-                        start=True,
-                        stop=True,
-                    )
-                    nc.vector.tensor_tensor(out=x[:, cols], in0=acc[:], in1=b1b[:, cols], op=ALU.add)
-                g = gp.tile([P, F], F32, tag="g")
-                s1 = sm.tile([P, 1], F32, tag="s1")
-                nc.scalar.activation(out=g[:], in_=x[:], func=ACT.Gelu, accum_out=s1[:])
-                nm = sm.tile([P, 1], F32, tag="nm")
-                nc.gpsimd.tensor_scalar(out=nm[:], in0=s1[:], scalar1=-1.0 / F, scalar2=0.0, op0=ALU.mult, op1=ALU.add)
-                junk = jp.tile([P, F], BF16, tag="junk")
-                ss = sm.tile([P, 1], F32, tag="ss")
-                nc.scalar.activation(out=junk[:], in_=g[:], func=ACT.Square, bias=nm[:], accum_out=ss[:])
-                rstd = rstd_of(ss, 1.0 / F, "a")
-                nc.vector.tensor_scalar(out=g[:], in0=g[:], scalar1=nm[:], scalar2=rstd[:], op0=ALU.add, op1=ALU.mult)
-                n_tiles.append(g)
-            return n_tiles
-
-        def stage_hq(n_tiles):
-            hb = hp.tile([P, 8, BLK], BF16, tag="hb")
-            for ct in range(8):
-                ht = ps.tile([P, BLK], F32, tag="ht", bufs=2)
-                for j in range(TB):
-                    nc.tensor.transpose(ht[:, P * j : P * (j + 1)], n_tiles[j][:, P * ct : P * (ct + 1)], ident[:])
-                nc.scalar.activation(
-                    out=hb[:, ct, :],
-                    in_=ht[:],
-                    func=ACT.Identity,
-                    scale=gb_col[:, ct : ct + 1],
-                    bias=gb_col[:, 8 + ct : 9 + ct],
-                )
-            hg = hp.tile([P, 2, BLK, 4], BF16, tag="hg", align_bytes=64)
-            hc = hp.tile([P, 2, BLK], U32, tag="hc", align_bytes=64)
-            hs = hp.tile([P, 2, BLK], U8, tag="hs", align_bytes=64)
-            for c in range(2):
-                regroup(nc, hg[:, c], hb[:, 4 * c : 4 * c + 4, :])
-            for c in range(2):
-                nc.vector.quantize_mx(
-                    out=hc[:, c, :].bitcast(FP8X4),
-                    scales=hs[:, c, :],
-                    in_=hg[:, c].rearrange("p w t -> p (w t)"),
-                )
-            return hc, hs
-
-        def stage_out(b, hc, hs):
-            o = ob.tile([P, TB, D], F32, tag="o")
-            for j in range(TB):
-                tok = slice(P * j, P * (j + 1))
-                y = ps.tile([P, D], F32, tag="y", bufs=2)
-                for c in range(2):
-                    nc.tensor.matmul_mx(
-                        out=y[:],
-                        lhsT=hc[:, c, tok].bitcast(FP8X4),
-                        lhsT_scale=hs[:, c, tok],
-                        rhs=w2c[:, c, :].bitcast(FP8X4),
-                        rhs_scale=w2s[:, c, :],
-                        start=(c == 0),
-                        stop=(c == 1),
-                    )
-                x2 = op.tile([P, D], F32, tag="x2")
-                s2 = sm.tile([P, 1], F32, tag="s2")
-                nc.vector.scalar_tensor_tensor(
-                    out=x2[:], in0=y[:], scalar=1.0, in1=b2b[:], op0=ALU.mult, op1=ALU.add, accum_out=s2[:]
-                )
-                nm2 = sm.tile([P, 1], F32, tag="nm2")
-                nc.gpsimd.tensor_scalar(out=nm2[:], in0=s2[:], scalar1=-1.0 / D, scalar2=0.0, op0=ALU.mult, op1=ALU.add)
-                junk2 = jp.tile([P, D], BF16, tag="junk2")
-                ss2 = sm.tile([P, 1], F32, tag="ss2")
-                nc.scalar.activation(out=junk2[:], in_=x2[:], func=ACT.Square, bias=nm2[:], accum_out=ss2[:])
-                rstd2 = rstd_of(ss2, 1.0 / D, "b")
-                t2 = op.tile([P, D], F32, tag="t2")
-                nc.vector.scalar_tensor_tensor(
-                    out=t2[:], in0=x2[:], scalar=nm2[:], in1=g2b[:], op0=ALU.add, op1=ALU.mult
-                )
-                nc.vector.scalar_tensor_tensor(
-                    out=o[:, j, :], in0=t2[:], scalar=rstd2[:], in1=be2b[:], op0=ALU.mult, op1=ALU.add
-                )
-            nc.sync.dma_start(
-                out=out[BLK * b : BLK * (b + 1), :].rearrange("(p j) d -> p (j d)", j=TB),
-                in_=o[:].rearrange("p j d -> p (j d)"),
-            )
-
-        for b in range(NBLK):
-            if b + 2 < NBLK:
-                load_z(b + 2)
-            zc, zs = stage_z(b)
-            n_tiles = stage_hidden(zc, zs)
+        for b in range(nb + 1):
+            cur, prv, nxt = b < nb, b >= 1, b + 1 < nb
+            if b + 3 < nb:
+                load_z(b + 3)
+            if nxt and b > 0:
+                zo(b + 1)
+            if cur:
+                nt = NT[b]
+                for j in range(nt):
+                    mm1_bias(b, j)
+                    gelu(b, j)
+                    if j >= 1:
+                        squares(b, j - 1)
+                squares(b, nt - 1)
             if b == 0:
-                prep_w2()
-            hc, hs = stage_hq(n_tiles)
-            stage_out(b, hc, hs)
+                late_setup()
+                zo(1)
+            if prv:
+                for c in range(2):
+                    h_regroup(b - 1, c)
+                for c in range(2):
+                    h_quant(b - 1, c)
+            n_list = [(norm, b, j) for j in range(NT[b])] if cur else []
+            o_list = [(mm2_bias, b - 1, j) for j in range(NT[b - 1])] if prv else []
+            seq = n_list[: len(n_list) // 2] + o_list[: len(o_list) // 2]
+            ra, rb = n_list[len(n_list) // 2 :], o_list[len(o_list) // 2 :]
+            for i in range(max(len(ra), len(rb))):
+                seq.extend(ra[i : i + 1])
+                seq.extend(rb[i : i + 1])
+            for f, bb, j in seq:
+                f(bb, j)
+            s_list = [(squares2, b - 1, j) for j in range(NT[b - 1])] if prv else []
+            a_list = [(t_affine, b, ct) for ct in range(8)] if cur else []
+            seq = s_list[:-1] + a_list[:2] + s_list[-1:] + a_list[2:]
+            for f, bb, j in seq:
+                f(bb, j)
+            if b + 2 < nb:
+                zT(b + 2)
+            if prv and cur:
+                for j in range(NT[b - 1]):
+                    centre_gain(b - 1, j)
+            if nxt:
+                zquant(b + 1)
+            if prv and cur:
+                for j in range(NT[b - 1]):
+                    scale_shift(b - 1, j)
+                store(b - 1)
+            if prv and not cur:
+                for j in range(NT[b - 1]):
+                    centre_gain(b - 1, j)
+                    scale_shift(b - 1, j)
+                    store_tile(b - 1, j)

@@ -16,7 +16,6 @@ B, D, F = 4096, 512, 1024
 EPS = 1e-5
 NT = [4, 4, 4, 4, 4, 4, 4, 4]
 FLOPS = 2 * B * D * F * 2
-NORM_ON_G = False
 A_ON_V = ((0, 1), (0, 3), (0, 5), (0, 7))
 
 
@@ -42,7 +41,7 @@ def tile_emaaggregator_pa_t_kernel(tc, z, W1, b1, g1, be1, W2, b2, g2, be2, out)
         hp = ctx.enter_context(tc.tile_pool(name="hp", bufs=2))
         op = ctx.enter_context(tc.tile_pool(name="op", bufs=5))
         ob = ctx.enter_context(tc.tile_pool(name="ob", bufs=2))
-        sm = ctx.enter_context(tc.tile_pool(name="sm", bufs=12))
+        sm = ctx.enter_context(tc.tile_pool(name="sm", bufs=3))
         ps = ctx.enter_context(tc.psum_pool(name="ps", bufs=4))
         ctx.enter_context(tc.manual_schedule())
         st = [dict() for b in range(nb)]
@@ -85,8 +84,10 @@ def tile_emaaggregator_pa_t_kernel(tc, z, W1, b1, g1, be1, W2, b2, g2, be2, out)
 
         ident = const.tile([P, P], F32)
         make_identity(nc, ident[:])
-        neg_half = const.tile([P, 1], F32)
+        neg_half = const.tile([P, 4], F32)
         nc.vector.memset(neg_half[:], -0.5)
+        eps_t = const.tile([P, 1], F32)
+        nc.vector.memset(eps_t[:], EPS)
         warm = const.tile([P, 1], F32)
         nc.vector.memset(warm[:], 0.0)
         warm2 = const.tile([P, 1], F32)
@@ -119,7 +120,7 @@ def tile_emaaggregator_pa_t_kernel(tc, z, W1, b1, g1, be1, W2, b2, g2, be2, out)
             zs = zq_pool.tile([P, nt * P], U8, tag="zs", align_bytes=64)
             nc.vector.quantize_mx(out=zc[:].bitcast(FP8X4), scales=zs[:], in_=st[b]["zg"][:].bitcast(BF16))
             st[b]["zc"], st[b]["zs"] = zc, zs
-            st[b]["x"], st[b]["g"], st[b]["s1"], st[b]["nm"], st[b]["rs"] = {}, {}, {}, {}, {}
+            st[b]["x"], st[b]["g"] = {}, {}
 
         def mm1_bias(b, j):
             tok = slice(P * j, P * (j + 1))
@@ -140,32 +141,31 @@ def tile_emaaggregator_pa_t_kernel(tc, z, W1, b1, g1, be1, W2, b2, g2, be2, out)
             st[b]["x"][j] = x
 
         def gelu(b, j):
+            if j == 0:
+                for key in ("s1", "ss", "nm", "ve", "rs"):
+                    col = sm.tile([P, 4], F32, tag=key)
+                    st[b][key] = col
             g = gp.tile([P, F], F32, tag="g")
-            s1 = sm.tile([P, 1], F32, tag="s1")
-            nc.scalar.activation(out=g[:], in_=st[b]["x"][j][:], func=ACT.Gelu, accum_out=s1[:])
-            st[b]["g"][j], st[b]["s1"][j] = g, s1
+            nc.scalar.activation(out=g[:], in_=st[b]["x"][j][:], func=ACT.Gelu, accum_out=st[b]["s1"][:, j : j + 1])
+            st[b]["g"][j] = g
 
-        def rstd_of(ss, scale, tag):
-            ve = sm.tile([P, 1], F32, tag=tag + "ve")
-            nc.gpsimd.tensor_scalar(out=ve[:], in0=ss[:], scalar1=scale, scalar2=EPS, op0=ALU.mult, op1=ALU.add)
-            rstd = sm.tile([P, 1], F32, tag=tag + "rs")
-            nc.gpsimd.tensor_tensor(out=rstd[:], in0=ve[:], in1=neg_half[:], op=ALU.pow)
-            return rstd
+        def rstd_cols(b, ss, ve, rs, lo, hi, n):
+            cols = slice(lo, hi)
+            if n == F:
+                nc.scalar.activation(out=st[b]["nm"][:, cols], in_=st[b]["s1"][:, cols], func=ACT.Identity, scale=-1.0 / F)
+            nc.scalar.activation(out=st[b][ve][:, cols], in_=st[b][ss][:, cols], func=ACT.Identity, scale=1.0 / (float(n) ** 3), bias=eps_t[:])
+            nc.gpsimd.tensor_tensor(out=st[b][rs][:, cols], in0=st[b][ve][:, cols], in1=neg_half[:, cols], op=ALU.pow)
 
         def squares(b, j):
-            s1 = st[b]["s1"][j]
-            nm = sm.tile([P, 1], F32, tag="nm")
-            nc.gpsimd.tensor_scalar(out=nm[:], in0=s1[:], scalar1=-1.0 / F, scalar2=0.0, op0=ALU.mult, op1=ALU.add)
             junk = jp.tile([P, F], BF16, tag="junk")
-            ss = sm.tile([P, 1], F32, tag="ss")
-            nc.scalar.activation(out=junk[:], in_=st[b]["g"][j][:], func=ACT.Square, scale=-float(F), bias=s1[:], accum_out=ss[:])
-            st[b]["nm"][j] = nm
-            st[b]["rs"][j] = rstd_of(ss, 1.0 / (float(F) ** 3), "a")
+            nc.scalar.activation(
+                out=junk[:], in_=st[b]["g"][j][:], func=ACT.Square, scale=-float(F),
+                bias=st[b]["s1"][:, j : j + 1], accum_out=st[b]["ss"][:, j : j + 1],
+            )
 
         def norm(b, j):
             g = st[b]["g"][j]
-            eng = nc.gpsimd if NORM_ON_G else nc.vector
-            eng.tensor_scalar(out=g[:], in0=g[:], scalar1=st[b]["nm"][j][:], scalar2=st[b]["rs"][j][:], op0=ALU.add, op1=ALU.mult)
+            nc.vector.tensor_scalar(out=g[:], in0=g[:], scalar1=st[b]["nm"][:, j : j + 1], scalar2=st[b]["rs"][:, j : j + 1], op0=ALU.add, op1=ALU.mult)
 
         def t_affine(b, ct):
             nt = NT[b]
@@ -208,7 +208,10 @@ def tile_emaaggregator_pa_t_kernel(tc, z, W1, b1, g1, be1, W2, b2, g2, be2, out)
                 st[b]["hc"], st[b]["hs"] = hc_new, hs_new
                 o_new = ob.tile([P, nt, D], F32, tag="o")
                 st[b]["o"] = o_new
-                st[b]["x2"], st[b]["s2"], st[b]["nm2"], st[b]["rs2"], st[b]["t2"] = {}, {}, {}, {}, {}
+                st[b]["x2"], st[b]["t2"] = {}, {}
+                for key in ("s2", "ss2", "nm2", "ve2", "rs2"):
+                    col = sm.tile([P, 4], F32, tag=key)
+                    st[b][key] = col
             nc.vector.quantize_mx(
                 out=st[b]["hc"][:, c, :].bitcast(FP8X4),
                 scales=st[b]["hs"][:, c, :],
@@ -229,25 +232,27 @@ def tile_emaaggregator_pa_t_kernel(tc, z, W1, b1, g1, be1, W2, b2, g2, be2, out)
                     stop=(c == 1),
                 )
             x2 = op.tile([P, D], F32, tag="x2")
-            s2 = sm.tile([P, 1], F32, tag="s2")
-            nc.vector.scalar_tensor_tensor(out=x2[:], in0=y[:], scalar=1.0, in1=b2b[:], op0=ALU.mult, op1=ALU.add, accum_out=s2[:])
-            nm2 = sm.tile([P, 1], F32, tag="nm2")
-            nc.gpsimd.tensor_scalar(out=nm2[:], in0=s2[:], scalar1=-1.0 / D, scalar2=0.0, op0=ALU.mult, op1=ALU.add)
-            st[b]["x2"][j], st[b]["s2"][j], st[b]["nm2"][j] = x2, s2, nm2
+            nc.vector.scalar_tensor_tensor(out=x2[:], in0=y[:], scalar=1.0, in1=b2b[:], op0=ALU.mult, op1=ALU.add, accum_out=st[b]["s2"][:, j : j + 1])
+            st[b]["x2"][j] = x2
+
+        def neg_mean2(b):
+            nt = NT[b]
+            nc.vector.tensor_scalar(out=st[b]["nm2"][:, 0:nt], in0=st[b]["s2"][:, 0:nt], scalar1=-1.0 / D, scalar2=None, op0=ALU.mult)
 
         def squares2(b, j):
             junk2 = jp.tile([P, D], BF16, tag="junk2")
-            ss2 = sm.tile([P, 1], F32, tag="ss2")
-            nc.scalar.activation(out=junk2[:], in_=st[b]["x2"][j][:], func=ACT.Square, scale=-float(D), bias=st[b]["s2"][j][:], accum_out=ss2[:])
-            st[b]["rs2"][j] = rstd_of(ss2, 1.0 / (float(D) ** 3), "b")
+            nc.scalar.activation(
+                out=junk2[:], in_=st[b]["x2"][j][:], func=ACT.Square, scale=-float(D),
+                bias=st[b]["s2"][:, j : j + 1], accum_out=st[b]["ss2"][:, j : j + 1],
+            )
 
         def centre_gain(b, j):
             t2 = op.tile([P, D], F32, tag="t2")
-            nc.vector.scalar_tensor_tensor(out=t2[:], in0=st[b]["x2"][j][:], scalar=st[b]["nm2"][j][:], in1=g2b[:], op0=ALU.add, op1=ALU.mult)
+            nc.vector.scalar_tensor_tensor(out=t2[:], in0=st[b]["x2"][j][:], scalar=st[b]["nm2"][:, j : j + 1], in1=g2b[:], op0=ALU.add, op1=ALU.mult)
             st[b]["t2"][j] = t2
 
         def scale_shift(b, j):
-            nc.vector.scalar_tensor_tensor(out=st[b]["o"][:, j, :], in0=st[b]["t2"][j][:], scalar=st[b]["rs2"][j][:], in1=be2b[:], op0=ALU.mult, op1=ALU.add)
+            nc.vector.scalar_tensor_tensor(out=st[b]["o"][:, j, :], in0=st[b]["t2"][j][:], scalar=st[b]["rs2"][:, j : j + 1], in1=be2b[:], op0=ALU.mult, op1=ALU.add)
 
         def store(b):
             nt = NT[b]
@@ -316,7 +321,10 @@ def tile_emaaggregator_pa_t_kernel(tc, z, W1, b1, g1, be1, W2, b2, g2, be2, out)
                     gelu(b, j)
                     if j >= 1:
                         squares(b, j - 1)
+                    if j == nt // 2 and nt >= 2:
+                        rstd_cols(b, "ss", "ve", "rs", 0, nt // 2, F)
                 squares(b, nt - 1)
+                rstd_cols(b, "ss", "ve", "rs", nt // 2, nt, F)
             if b == 0:
                 late_setup()
                 zo(1)
@@ -336,8 +344,18 @@ def tile_emaaggregator_pa_t_kernel(tc, z, W1, b1, g1, be1, W2, b2, g2, be2, out)
                 f(bb, j)
             s_list = [(squares2, b - 1, j) for j in range(NT[b - 1])] if prv else []
             a_list = [(t_affine, b, ct) for ct in range(8)] if cur else []
-            seq = s_list[:-1] + a_list[:2] + s_list[-1:] + a_list[2:]
+            half = len(s_list) // 2
+            for f, bb, j in s_list[:half]:
+                f(bb, j)
+            if prv and half > 0:
+                rstd_cols(b - 1, "ss2", "ve2", "rs2", 0, half, D)
+            seq = s_list[half:-1] + a_list[:2] + s_list[-1:]
             for f, bb, j in seq:
+                f(bb, j)
+            if prv:
+                rstd_cols(b - 1, "ss2", "ve2", "rs2", half, NT[b - 1], D)
+                neg_mean2(b - 1)
+            for f, bb, j in a_list[2:]:
                 f(bb, j)
             if b + 2 < nb:
                 zT(b + 2)

@@ -14,13 +14,109 @@ ALU = mybir.AluOpType
 P = 128
 B, D, F = 4096, 512, 1024
 EPS = 1e-5
-NT = [4, 4, 4, 4, 4, 4, 4, 4]
+NT = 4
+BLK = NT * P
+NB = B // BLK
 FLOPS = 2 * B * D * F * 2
-A_ON_V = ((0, 1), (0, 3), (0, 5), (0, 7))
+EDGE = (0, NB - 1)
+LAG = 8
+
+PERIOD = (
+    ("Rg", -2, 1),
+    ("B", -1, 7),
+    ("zo", 1, 0),
+    ("Sq", -1, 1),
+    ("Q", -2, 0),
+    ("Q", -2, 1),
+    ("st1", -1, 0),
+    ("O3", -3, 3),
+    ("w2q", -2, 1),
+    ("mm1", 0, 1),
+    ("B", 0, 0),
+    ("O4", -3, 3),
+    ("store", -3, 0),
+    ("mm2", -2, 0),
+    ("mm1", 0, 2),
+    ("w2p", -1, 0),
+    ("Ng", -1, 1),
+    ("B", 0, 1),
+    ("Ge", -1, 2),
+    ("Ge", -1, 3),
+    ("mm2", -2, 1),
+    ("Ng", -1, 0),
+    ("Sq", -1, 2),
+    ("O1", -2, 0),
+    ("B", 0, 2),
+    ("mm2", -2, 2),
+    ("Sq", -1, 3),
+    ("mm1", 0, 3),
+    ("O1", -2, 1),
+    ("O1", -2, 2),
+    ("gbs", -1, 0),
+    ("B", 0, 3),
+    ("st1", -1, 1),
+    ("Ng", -1, 2),
+    ("Ng", -1, 3),
+    ("Ge", 0, 0),
+    ("O2", -2, 0),
+    ("w1p", 1, 0),
+    ("Sq", 0, 0),
+    ("mm2", -2, 3),
+    ("O1", -2, 3),
+    ("nm2", -2, 0),
+    ("O3", -2, 0),
+    ("O2", -2, 1),
+    ("O2", -2, 2),
+    ("zq", 1, 0),
+    ("zT", 2, 1),
+    ("w1p", 1, 1),
+    ("st2", -2, 0),
+    ("w2p", -1, 1),
+    ("T", -1, 0),
+    ("nm2", -2, 1),
+    ("O2", -2, 3),
+    ("O3", -2, 1),
+    ("T", -1, 1),
+    ("T", -1, 3),
+    ("T", -1, 2),
+    ("A", -1, 0),
+    ("O3", -2, 2),
+    ("T", -1, 4),
+    ("st2", -2, 1),
+    ("Av", -1, 3),
+    ("A", -1, 1),
+    ("T", -1, 6),
+    ("A", -1, 2),
+    ("O4", -2, 1),
+    ("T", -1, 5),
+    ("w2q", -1, 0),
+    ("w1q", 1, 0),
+    ("T", -1, 7),
+    ("A", -1, 4),
+    ("O4", -2, 0),
+    ("Rg", -1, 0),
+    ("mm1", 0, 4),
+    ("Av", -1, 7),
+    ("A", -1, 6),
+    ("mm1", 0, 5),
+    ("zT", 2, 0),
+    ("ld", 3, 0),
+    ("w1q", 1, 1),
+    ("O4", -2, 2),
+    ("A", -1, 5),
+    ("B", 0, 4),
+    ("mm1", 0, 6),
+    ("mm1", 0, 7),
+    ("zov", 2, 1),
+    ("Ge", 0, 1),
+    ("mm1", 1, 0),
+    ("B", 0, 5),
+    ("B", 0, 6),
+)
 
 
-def regroup(nc, dst, src):
-    nc.vector.tensor_copy(
+def regroup(eng, dst, src):
+    eng.tensor_copy(
         out=dst.rearrange("p (c i) t -> p c t i", i=4),
         in_=src.rearrange("p t (c i) -> p c t i", i=4),
     )
@@ -28,199 +124,218 @@ def regroup(nc, dst, src):
 
 def tile_emaaggregator_pa_t_kernel(tc, z, W1, b1, g1, be1, W2, b2, g2, be2, out):
     nc = tc.nc
-    nb = len(NT)
-    tok0 = [P * sum(NT[:b]) for b in range(nb)]
     with ExitStack() as ctx:
         const = ctx.enter_context(tc.tile_pool(name="const", bufs=1))
-        wst = ctx.enter_context(tc.tile_pool(name="wst", bufs=1))
         zin = ctx.enter_context(tc.tile_pool(name="zin", bufs=4))
-        zq_pool = ctx.enter_context(tc.tile_pool(name="zq", bufs=2))
+        zqp = ctx.enter_context(tc.tile_pool(name="zqp", bufs=3))
         xp = ctx.enter_context(tc.tile_pool(name="xp", bufs=4))
-        gp = ctx.enter_context(tc.tile_pool(name="gp", bufs=8))
+        gp = ctx.enter_context(tc.tile_pool(name="gp", bufs=12))
         jp = ctx.enter_context(tc.tile_pool(name="jp", bufs=2))
         hp = ctx.enter_context(tc.tile_pool(name="hp", bufs=2))
-        op = ctx.enter_context(tc.tile_pool(name="op", bufs=5))
+        op = ctx.enter_context(tc.tile_pool(name="op", bufs=6))
         ob = ctx.enter_context(tc.tile_pool(name="ob", bufs=2))
         sm = ctx.enter_context(tc.tile_pool(name="sm", bufs=3))
         ps = ctx.enter_context(tc.psum_pool(name="ps", bufs=4))
         ctx.enter_context(tc.manual_schedule())
-        st = [dict() for b in range(nb)]
+        st = [dict() for b in range(NB)]
 
-        def load_z(b):
-            nt = NT[b]
-            z_sb = zin.tile([P, nt * D], BF16, tag="z")
-            nc.sync.dma_start(
-                out=z_sb[:],
-                in_=z[tok0[b] : tok0[b] + nt * P, :].rearrange("(p j) k -> p (j k)", j=nt),
-            )
+        def load_z(b, i):
+            z_sb = zin.tile([P, NT * D], BF16, tag="z")
+            nc.sync.dma_start(out=z_sb[:], in_=z[BLK * b : BLK * (b + 1), :].rearrange("(p j) k -> p (j k)", j=NT))
             st[b]["z"] = z_sb
 
-        load_z(0)
-        w1r0 = wst.tile([P, 4, 512], BF16)
-        w1r1 = wst.tile([P, 4, 512], BF16)
-        w1r = [w1r0, w1r1]
+        load_z(0, 0)
+        w1r = hp.tile([P, 2, 4, 512], BF16, tag="hb")
         for h in range(2):
             for u in range(2):
                 nc.sync.dma_start(
-                    out=w1r[h][:, 2 * u : 2 * u + 2, :],
+                    out=w1r[:, h, 2 * u : 2 * u + 2, :],
                     in_=W1[256 * u : 256 * (u + 1), 512 * h : 512 * (h + 1)].rearrange("(q e) c -> q e c", e=2),
                 )
         gb_rows = const.tile([P, P], BF16)
         nc.vector.memset(gb_rows[:], 0.0)
         nc.scalar.dma_start(out=gb_rows[0:8, :], in_=g1.rearrange("(r c) -> r c", c=P))
         nc.scalar.dma_start(out=gb_rows[8:16, :], in_=be1.rearrange("(r c) -> r c", c=P))
+        g2_rows = const.tile([P, 2 * D], BF16)
+        nc.vector.memset(g2_rows[:], 0.0)
+        nc.scalar.dma_start(out=g2_rows[0:1, 0:D], in_=g2.rearrange("(o c) -> o c", o=1))
+        nc.scalar.dma_start(out=g2_rows[0:1, D : 2 * D], in_=be2.rearrange("(o c) -> o c", o=1))
         b1b = const.tile([P, F], BF16)
         nc.sync.dma_start(out=b1b[:], in_=b1.partition_broadcast(P))
-        load_z(1)
-        w2r = wst.tile([P, 8, D], BF16)
+        load_z(1, 0)
+        w2r = hp.tile([P, 8, D], BF16, tag="hb")
         nc.sync.dma_start(out=w2r[:], in_=W2.rearrange("(ct p) n -> p ct n", p=P))
         b2b = const.tile([P, D], BF16)
         nc.sync.dma_start(out=b2b[:], in_=b2.partition_broadcast(P))
-        g2b = const.tile([P, D], BF16)
-        nc.sync.dma_start(out=g2b[:], in_=g2.partition_broadcast(P))
-        be2b = const.tile([P, D], BF16)
-        nc.sync.dma_start(out=be2b[:], in_=be2.partition_broadcast(P))
-        load_z(2)
+        load_z(2, 0)
 
         ident = const.tile([P, P], F32)
         make_identity(nc, ident[:])
+        ones = const.tile([P, P], BF16)
+        nc.vector.memset(ones[:], 1.0)
         neg_half = const.tile([P, 4], F32)
         nc.vector.memset(neg_half[:], -0.5)
         eps_t = const.tile([P, 1], F32)
         nc.vector.memset(eps_t[:], EPS)
         warm = const.tile([P, 1], F32)
-        nc.vector.memset(warm[:], 0.0)
-        warm2 = const.tile([P, 1], F32)
-        nc.scalar.activation(out=warm2[:], in_=warm[:], func=ACT.Gelu)
+        nc.scalar.activation(out=warm[:], in_=eps_t[:], func=ACT.Gelu)
 
-        def zT(b):
-            nt = NT[b]
-            zw = st[b]["z"][:].bitcast(F32)
-            st[b]["zt"] = []
-            for j0 in range(0, nt, 2):
-                nj = min(2, nt - j0)
-                zt = ps.tile([P, nj, 2, P], F32, tag="Y")
-                for jj in range(nj):
-                    for u in range(2):
-                        c0 = (j0 + jj) * 256 + u * P
-                        nc.tensor.transpose(zt[:, jj, u, :], zw[:, c0 : c0 + P], ident[:])
-                st[b]["zt"].append((j0, nj, zt))
+        w1g = hp.tile([P, F, 4], BF16, tag="hg", align_bytes=64)
+        w1c = const.tile([P, F], U32, align_bytes=64)
+        w1s = const.tile([P, F], U8, align_bytes=64)
+        w2g = hp.tile([P, 2, D, 4], BF16, tag="hg", align_bytes=64)
+        w2c = const.tile([P, 2, D], U32, align_bytes=64)
+        w2s = const.tile([P, 2, D], U8, align_bytes=64)
+        gb_col = const.tile([P, 16], F32)
+        g2ps = ps.tile([P, 2 * D], BF16, tag="C", bufs=1)
 
-        def zo(b):
-            nt = NT[b]
-            zg = zq_pool.tile([P, nt * P * 2], F32, tag="zg", align_bytes=64)
-            zgv = zg[:].rearrange("q (j t u) -> q j t u", j=nt, u=2)
-            for j0, nj, zt in st[b]["zt"]:
-                nc.scalar.copy(out=zgv[:, j0 : j0 + nj, :, :], in_=zt[:].rearrange("q j u t -> q j t u"))
-            st[b]["zg"] = zg
-
-        def zquant(b):
-            nt = NT[b]
-            zc = zq_pool.tile([P, nt * P], U32, tag="zc", align_bytes=64)
-            zs = zq_pool.tile([P, nt * P], U8, tag="zs", align_bytes=64)
-            nc.vector.quantize_mx(out=zc[:].bitcast(FP8X4), scales=zs[:], in_=st[b]["zg"][:].bitcast(BF16))
-            st[b]["zc"], st[b]["zs"] = zc, zs
-            st[b]["x"], st[b]["g"] = {}, {}
-
-        def mm1_bias(b, j):
-            tok = slice(P * j, P * (j + 1))
-            x = xp.tile([P, F], F32, tag="x")
-            for h in range(2):
-                cols = slice(512 * h, 512 * (h + 1))
-                acc = ps.tile([P, 512], F32, tag="X")
-                nc.tensor.matmul_mx(
-                    out=acc[:],
-                    lhsT=st[b]["zc"][:, tok].bitcast(FP8X4),
-                    lhsT_scale=st[b]["zs"][:, tok],
-                    rhs=w1c[:, cols].bitcast(FP8X4),
-                    rhs_scale=w1s[:, cols],
-                    start=True,
-                    stop=True,
-                )
-                nc.vector.tensor_tensor(out=x[:, cols], in0=acc[:], in1=b1b[:, cols], op=ALU.add)
-            st[b]["x"][j] = x
-
-        def gelu(b, j):
-            if j == 0:
-                for key in ("s1", "ss", "nm", "ve", "rs"):
+        def cols_of(b, keys):
+            for key in keys:
+                if key not in st[b]:
                     col = sm.tile([P, 4], F32, tag=key)
                     st[b][key] = col
+
+        def zT(b, i):
+            zw = st[b]["z"][:].bitcast(F32)
+            zt = ps.tile([P, 2, 2, P], F32, tag="Y", bufs=3)
+            for jj in range(2):
+                for u in range(2):
+                    c0 = (2 * i + jj) * 256 + u * P
+                    nc.tensor.transpose(zt[:, jj, u, :], zw[:, c0 : c0 + P], ident[:])
+            st[b]["zt", i] = zt
+
+        def zo_on(copy, b, i):
+            if "zg" not in st[b]:
+                zg = zqp.tile([P, NT * P * 2], F32, tag="zg", align_bytes=64)
+                st[b]["zg"] = zg
+            zgv = st[b]["zg"][:].rearrange("q (j t u) -> q j t u", j=NT, u=2)
+            copy(out=zgv[:, 2 * i : 2 * i + 2, :, :], in_=st[b]["zt", i][:].rearrange("q j u t -> q j t u"))
+
+        def zo(b, i):
+            zo_on(nc.scalar.copy, b, i)
+
+        def zov(b, i):
+            zo_on(nc.vector.tensor_copy, b, i)
+
+        def zq(b, i):
+            zc = zqp.tile([P, BLK], U32, tag="zc", align_bytes=64)
+            zs = zqp.tile([P, BLK], U8, tag="zs", align_bytes=64)
+            nc.vector.quantize_mx(out=zc[:].bitcast(FP8X4), scales=zs[:], in_=st[b]["zg"][:].bitcast(BF16))
+            st[b]["zc"], st[b]["zs"] = zc, zs
+
+        def mm1(b, i):
+            j, h = i // 2, i % 2
+            tok = slice(P * j, P * (j + 1))
+            cols = slice(512 * h, 512 * (h + 1))
+            acc = ps.tile([P, 512], F32, tag="X")
+            nc.tensor.matmul_mx(
+                out=acc[:],
+                lhsT=st[b]["zc"][:, tok].bitcast(FP8X4),
+                lhsT_scale=st[b]["zs"][:, tok],
+                rhs=w1c[:, cols].bitcast(FP8X4),
+                rhs_scale=w1s[:, cols],
+                start=True,
+                stop=True,
+            )
+            st[b]["acc", i] = acc
+
+        def Bi(b, i):
+            j, h = i // 2, i % 2
+            cols = slice(512 * h, 512 * (h + 1))
+            if h == 0:
+                x = xp.tile([P, F], F32, tag="x")
+                st[b]["x", j] = x
+            nc.vector.tensor_tensor(out=st[b]["x", j][:, cols], in0=st[b]["acc", i][:], in1=b1b[:, cols], op=ALU.add)
+
+        def Ge(b, j):
+            cols_of(b, ("s1", "ss", "nm", "ve", "rs"))
             g = gp.tile([P, F], F32, tag="g")
-            nc.scalar.activation(out=g[:], in_=st[b]["x"][j][:], func=ACT.Gelu, accum_out=st[b]["s1"][:, j : j + 1])
-            st[b]["g"][j] = g
+            nc.scalar.activation(out=g[:], in_=st[b]["x", j][:], func=ACT.Gelu, accum_out=st[b]["s1"][:, j : j + 1])
+            st[b]["g", j] = g
 
-        def rstd_cols(b, ss, ve, rs, lo, hi, n):
-            cols = slice(lo, hi)
-            if n == F:
-                nc.scalar.activation(out=st[b]["nm"][:, cols], in_=st[b]["s1"][:, cols], func=ACT.Identity, scale=-1.0 / F)
-            nc.scalar.activation(out=st[b][ve][:, cols], in_=st[b][ss][:, cols], func=ACT.Identity, scale=1.0 / (float(n) ** 3), bias=eps_t[:])
-            nc.gpsimd.tensor_tensor(out=st[b][rs][:, cols], in0=st[b][ve][:, cols], in1=neg_half[:, cols], op=ALU.pow)
-
-        def squares(b, j):
+        def Sq(b, j):
             junk = jp.tile([P, F], BF16, tag="junk")
             nc.scalar.activation(
-                out=junk[:], in_=st[b]["g"][j][:], func=ACT.Square, scale=-float(F),
+                out=junk[:], in_=st[b]["g", j][:], func=ACT.Square, scale=-float(F),
                 bias=st[b]["s1"][:, j : j + 1], accum_out=st[b]["ss"][:, j : j + 1],
             )
 
-        def norm(b, j):
-            g = st[b]["g"][j]
-            nc.vector.tensor_scalar(out=g[:], in0=g[:], scalar1=st[b]["nm"][:, j : j + 1], scalar2=st[b]["rs"][:, j : j + 1], op0=ALU.add, op1=ALU.mult)
+        def rstd_cols(b, ss, ve, rs, cols, n):
+            nc.scalar.activation(out=st[b][ve][:, cols], in_=st[b][ss][:, cols], func=ACT.Identity, scale=1.0 / (float(n) ** 3), bias=eps_t[:])
+            nc.gpsimd.tensor_tensor(out=st[b][rs][:, cols], in0=st[b][ve][:, cols], in1=neg_half[:, cols], op=ALU.pow)
 
-        def t_affine(b, ct):
-            nt = NT[b]
-            if ct == 0:
-                hb_new = hp.tile([P, 8, nt * P], BF16, tag="hb")
-                st[b]["hb"] = hb_new
-            ht = ps.tile([P, nt * P], F32, tag="X")
-            for j in range(nt):
-                nc.tensor.transpose(ht[:, P * j : P * (j + 1)], st[b]["g"][j][:, P * ct : P * (ct + 1)], ident[:])
-            if (b, ct) in A_ON_V:
-                nc.vector.tensor_scalar(
-                    out=st[b]["hb"][:, ct, :],
-                    in0=ht[:],
-                    scalar1=gb_col[:, ct : ct + 1],
-                    scalar2=gb_col[:, 8 + ct : 9 + ct],
-                    op0=ALU.mult,
-                    op1=ALU.add,
-                )
-            else:
-                nc.scalar.activation(
-                    out=st[b]["hb"][:, ct, :],
-                    in_=ht[:],
-                    func=ACT.Identity,
-                    scale=gb_col[:, ct : ct + 1],
-                    bias=gb_col[:, 8 + ct : 9 + ct],
-                )
+        def st1(b, i):
+            cols = slice(2 * i, 2 * i + 2)
+            nc.scalar.activation(out=st[b]["nm"][:, cols], in_=st[b]["s1"][:, cols], func=ACT.Identity, scale=-1.0 / F)
+            rstd_cols(b, "ss", "ve", "rs", cols, F)
 
-        def h_regroup(b, c):
-            nt = NT[b]
-            if c == 0:
-                hg_new = hp.tile([P, 2, nt * P, 4], BF16, tag="hg", align_bytes=64)
-                st[b]["hg"] = hg_new
-            regroup(nc, st[b]["hg"][:, c], st[b]["hb"][:, 4 * c : 4 * c + 4, :])
+        def norm_on(eng, b, j):
+            g = st[b]["g", j]
+            eng.tensor_scalar(out=g[:], in0=g[:], scalar1=st[b]["nm"][:, j : j + 1], scalar2=st[b]["rs"][:, j : j + 1], op0=ALU.add, op1=ALU.mult)
+            st[b]["n", j] = g
 
-        def h_quant(b, c):
-            nt = NT[b]
-            if c == 0:
-                hc_new = hp.tile([P, 2, nt * P], U32, tag="hc", align_bytes=64)
-                hs_new = hp.tile([P, 2, nt * P], U8, tag="hs", align_bytes=64)
-                st[b]["hc"], st[b]["hs"] = hc_new, hs_new
-                o_new = ob.tile([P, nt, D], F32, tag="o")
-                st[b]["o"] = o_new
-                st[b]["x2"], st[b]["t2"] = {}, {}
-                for key in ("s2", "ss2", "nm2", "ve2", "rs2"):
-                    col = sm.tile([P, 4], F32, tag=key)
-                    st[b][key] = col
+        def N(b, j):
+            norm_on(nc.vector, b, j)
+
+        def Ng(b, j):
+            norm_on(nc.vector if b in EDGE else nc.gpsimd, b, j)
+
+        def T(b, ct):
+            ht = ps.tile([P, BLK], F32, tag="X")
+            for j in range(NT):
+                nc.tensor.transpose(ht[:, P * j : P * (j + 1)], st[b]["n", j][:, P * ct : P * (ct + 1)], ident[:])
+            st[b]["ht", ct] = ht
+
+        def hb_of(b):
+            if "hb" not in st[b]:
+                hb = hp.tile([P, 8, BLK], BF16, tag="hb")
+                st[b]["hb"] = hb
+            return st[b]["hb"]
+
+        def A(b, ct):
+            nc.scalar.activation(
+                out=hb_of(b)[:, ct, :], in_=st[b]["ht", ct][:], func=ACT.Identity,
+                scale=gb_col[:, ct : ct + 1], bias=gb_col[:, 8 + ct : 9 + ct],
+            )
+
+        def Av(b, ct):
+            nc.vector.tensor_scalar(
+                out=hb_of(b)[:, ct, :], in0=st[b]["ht", ct][:],
+                scalar1=gb_col[:, ct : ct + 1], scalar2=gb_col[:, 8 + ct : 9 + ct], op0=ALU.mult, op1=ALU.add,
+            )
+
+        def hg_of(b):
+            if "hg" not in st[b]:
+                hg = hp.tile([P, 2, BLK, 4], BF16, tag="hg", align_bytes=64)
+                st[b]["hg"] = hg
+            return st[b]["hg"]
+
+        def R(b, c):
+            regroup(nc.vector, hg_of(b)[:, c], st[b]["hb"][:, 4 * c : 4 * c + 4, :])
+
+        def Rg(b, c):
+            if b in EDGE:
+                R(b, c)
+                return
+            nc.gpsimd.tensor_scalar(
+                out=hg_of(b)[:, c], in0=st[b]["hb"][:, 4 * c : 4 * c + 4, :].rearrange("p t w -> p w t"),
+                scalar1=1.0, scalar2=0.0, op0=ALU.mult, op1=ALU.add,
+            )
+
+        def Q(b, c):
+            if "hc" not in st[b]:
+                hc = hp.tile([P, 2, BLK], U32, tag="hc", align_bytes=64)
+                hs = hp.tile([P, 2, BLK], U8, tag="hs", align_bytes=64)
+                st[b]["hc"], st[b]["hs"] = hc, hs
             nc.vector.quantize_mx(
                 out=st[b]["hc"][:, c, :].bitcast(FP8X4),
                 scales=st[b]["hs"][:, c, :],
                 in_=st[b]["hg"][:, c].rearrange("p w t -> p (w t)"),
             )
 
-        def mm2_bias(b, j):
+        def mm2(b, j):
             tok = slice(P * j, P * (j + 1))
-            y = ps.tile([P, D], F32, tag="Y")
+            y = ps.tile([P, D], F32, tag="Y", bufs=3)
             for c in range(2):
                 nc.tensor.matmul_mx(
                     out=y[:],
@@ -231,145 +346,92 @@ def tile_emaaggregator_pa_t_kernel(tc, z, W1, b1, g1, be1, W2, b2, g2, be2, out)
                     start=(c == 0),
                     stop=(c == 1),
                 )
+            st[b]["y", j] = y
+
+        def O1(b, j):
+            cols_of(b, ("s2", "ss2", "nm2", "ve2", "rs2"))
             x2 = op.tile([P, D], F32, tag="x2")
-            nc.vector.scalar_tensor_tensor(out=x2[:], in0=y[:], scalar=1.0, in1=b2b[:], op0=ALU.mult, op1=ALU.add, accum_out=st[b]["s2"][:, j : j + 1])
-            st[b]["x2"][j] = x2
+            nc.vector.scalar_tensor_tensor(
+                out=x2[:], in0=st[b]["y", j][:], scalar=1.0, in1=b2b[:], op0=ALU.mult, op1=ALU.add,
+                accum_out=st[b]["s2"][:, j : j + 1],
+            )
+            st[b]["x2", j] = x2
 
-        def neg_mean2(b):
-            nt = NT[b]
-            nc.vector.tensor_scalar(out=st[b]["nm2"][:, 0:nt], in0=st[b]["s2"][:, 0:nt], scalar1=-1.0 / D, scalar2=None, op0=ALU.mult)
+        def nm2(b, i):
+            cols = slice(2 * i, 2 * i + 2)
+            nc.scalar.activation(out=st[b]["nm2"][:, cols], in_=st[b]["s2"][:, cols], func=ACT.Identity, scale=-1.0 / D)
 
-        def squares2(b, j):
+        def O2(b, j):
             junk2 = jp.tile([P, D], BF16, tag="junk2")
             nc.scalar.activation(
-                out=junk2[:], in_=st[b]["x2"][j][:], func=ACT.Square, scale=-float(D),
+                out=junk2[:], in_=st[b]["x2", j][:], func=ACT.Square, scale=-float(D),
                 bias=st[b]["s2"][:, j : j + 1], accum_out=st[b]["ss2"][:, j : j + 1],
             )
 
-        def centre_gain(b, j):
+        def st2(b, i):
+            rstd_cols(b, "ss2", "ve2", "rs2", slice(2 * i, 2 * i + 2), D)
+
+        def O3(b, j):
             t2 = op.tile([P, D], F32, tag="t2")
-            nc.vector.scalar_tensor_tensor(out=t2[:], in0=st[b]["x2"][j][:], scalar=st[b]["nm2"][:, j : j + 1], in1=g2b[:], op0=ALU.add, op1=ALU.mult)
-            st[b]["t2"][j] = t2
-
-        def scale_shift(b, j):
-            nc.vector.scalar_tensor_tensor(out=st[b]["o"][:, j, :], in0=st[b]["t2"][j][:], scalar=st[b]["rs2"][:, j : j + 1], in1=be2b[:], op0=ALU.mult, op1=ALU.add)
-
-        def store(b):
-            nt = NT[b]
-            nc.sync.dma_start(
-                out=out[tok0[b] : tok0[b] + nt * P, :].rearrange("(p j) d -> p (j d)", j=nt),
-                in_=st[b]["o"][:].rearrange("p j d -> p (j d)"),
+            nc.vector.scalar_tensor_tensor(
+                out=t2[:], in0=st[b]["x2", j][:], scalar=st[b]["nm2"][:, j : j + 1], in1=g2ps[:, 0:D], op0=ALU.add, op1=ALU.mult
             )
+            st[b]["t2", j] = t2
 
-        def store_tile(b, j):
-            nt = NT[b]
-            nc.sync.dma_start(
-                out=out[tok0[b] : tok0[b] + nt * P, :].rearrange("(p j) d -> p j d", j=nt)[:, j, :],
-                in_=st[b]["o"][:, j, :],
+        def O4(b, j):
+            if "o" not in st[b]:
+                o = ob.tile([P, NT, D], F32, tag="o")
+                st[b]["o"] = o
+            nc.vector.scalar_tensor_tensor(
+                out=st[b]["o"][:, j, :], in0=st[b]["t2", j][:], scalar=st[b]["rs2"][:, j : j + 1], in1=g2ps[:, D : 2 * D], op0=ALU.mult, op1=ALU.add
             )
-
-        zT(0)
-        zo(0)
-        w1g = wst.tile([P, F, 4], BF16, tag="wg", bufs=2, align_bytes=64)
-        w1c = const.tile([P, F], U32, align_bytes=64)
-        w1s = const.tile([P, F], U8, align_bytes=64)
-        w2g = wst.tile([P, 2, D, 4], BF16, tag="wg", bufs=2, align_bytes=64)
-        w2c = const.tile([P, 2, D], U32, align_bytes=64)
-        w2s = const.tile([P, 2, D], U8, align_bytes=64)
-        gb_col = const.tile([P, 16], F32)
-
-        def w1_quant(h):
-            cols = slice(512 * h, 512 * (h + 1))
-            nc.vector.quantize_mx(
-                out=w1c[:, cols].bitcast(FP8X4),
-                scales=w1s[:, cols],
-                in_=w1g[:, cols, :].rearrange("p w t -> p (w t)"),
-            )
-
-        regroup(nc, w1g[:, 0:512, :], w1r[0][:])
-        zquant(0)
-        w1_quant(0)
-        regroup(nc, w1g[:, 512:1024, :], w1r[1][:])
-        w1_quant(1)
-
-        def late_setup():
-            zT(1)
-            gb_f = const.tile([P, P], F32)
-            nc.vector.tensor_copy(out=gb_f[:], in_=gb_rows[:])
-            gb_ps = ps.tile([P, P], F32, tag="X")
-            nc.tensor.transpose(gb_ps[:], gb_f[:], ident[:])
-            nc.vector.tensor_copy(out=gb_col[:], in_=gb_ps[:, 0:16])
-            for c in range(2):
-                regroup(nc, w2g[:, c], w2r[:, 4 * c : 4 * c + 4, :])
-            for c in range(2):
-                nc.vector.quantize_mx(
-                    out=w2c[:, c, :].bitcast(FP8X4),
-                    scales=w2s[:, c, :],
-                    in_=w2g[:, c].rearrange("p w t -> p (w t)"),
+            if b == NB - 1:
+                nc.sync.dma_start(
+                    out=out[BLK * b : BLK * (b + 1), :].rearrange("(p j) d -> p j d", j=NT)[:, j, :], in_=st[b]["o"][:, j, :]
                 )
 
-        for b in range(nb + 1):
-            cur, prv, nxt = b < nb, b >= 1, b + 1 < nb
-            if b + 3 < nb:
-                load_z(b + 3)
-            if nxt and b > 0:
-                zo(b + 1)
-            if cur:
-                nt = NT[b]
-                for j in range(nt):
-                    mm1_bias(b, j)
-                    gelu(b, j)
-                    if j >= 1:
-                        squares(b, j - 1)
-                    if j == nt // 2 and nt >= 2:
-                        rstd_cols(b, "ss", "ve", "rs", 0, nt // 2, F)
-                squares(b, nt - 1)
-                rstd_cols(b, "ss", "ve", "rs", nt // 2, nt, F)
+        def store(b, i):
+            if b < NB - 1:
+                nc.sync.dma_start(
+                    out=out[BLK * b : BLK * (b + 1), :].rearrange("(p j) d -> p (j d)", j=NT),
+                    in_=st[b]["o"][:].rearrange("p j d -> p (j d)"),
+                )
+
+        def w1p(b, h):
             if b == 0:
-                late_setup()
-                zo(1)
-            if prv:
-                for c in range(2):
-                    h_regroup(b - 1, c)
-                for c in range(2):
-                    h_quant(b - 1, c)
-            n_list = [(norm, b, j) for j in range(NT[b])] if cur else []
-            o_list = [(mm2_bias, b - 1, j) for j in range(NT[b - 1])] if prv else []
-            seq = n_list[: len(n_list) // 2] + o_list[: len(o_list) // 2]
-            ra, rb = n_list[len(n_list) // 2 :], o_list[len(o_list) // 2 :]
-            for i in range(max(len(ra), len(rb))):
-                seq.extend(ra[i : i + 1])
-                seq.extend(rb[i : i + 1])
-            for f, bb, j in seq:
-                f(bb, j)
-            s_list = [(squares2, b - 1, j) for j in range(NT[b - 1])] if prv else []
-            a_list = [(t_affine, b, ct) for ct in range(8)] if cur else []
-            half = len(s_list) // 2
-            for f, bb, j in s_list[:half]:
-                f(bb, j)
-            if prv and half > 0:
-                rstd_cols(b - 1, "ss2", "ve2", "rs2", 0, half, D)
-            seq = s_list[half:-1] + a_list[:2] + s_list[-1:]
-            for f, bb, j in seq:
-                f(bb, j)
-            if prv:
-                rstd_cols(b - 1, "ss2", "ve2", "rs2", half, NT[b - 1], D)
-                neg_mean2(b - 1)
-            for f, bb, j in a_list[2:]:
-                f(bb, j)
-            if b + 2 < nb:
-                zT(b + 2)
-            if prv and cur:
-                for j in range(NT[b - 1]):
-                    centre_gain(b - 1, j)
-            if nxt:
-                zquant(b + 1)
-            if prv and cur:
-                for j in range(NT[b - 1]):
-                    scale_shift(b - 1, j)
-                store(b - 1)
-            if prv and not cur:
-                for j in range(NT[b - 1]):
-                    centre_gain(b - 1, j)
-                    scale_shift(b - 1, j)
-                    store_tile(b - 1, j)
+                cols = slice(512 * h, 512 * (h + 1))
+                regroup(nc.vector, w1g[:, cols, :], w1r[:, h])
+
+        def w1q(b, h):
+            if b == 0:
+                cols = slice(512 * h, 512 * (h + 1))
+                nc.vector.quantize_mx(out=w1c[:, cols].bitcast(FP8X4), scales=w1s[:, cols], in_=w1g[:, cols, :].rearrange("p w t -> p (w t)"))
+
+        def w2p(b, c):
+            if b == 0:
+                regroup(nc.vector, w2g[:, c], w2r[:, 4 * c : 4 * c + 4, :])
+
+        def w2q(b, c):
+            if b == 0:
+                nc.vector.quantize_mx(out=w2c[:, c, :].bitcast(FP8X4), scales=w2s[:, c, :], in_=w2g[:, c].rearrange("p w t -> p (w t)"))
+
+        def gbs(b, i):
+            if b == 0:
+                gb_f = const.tile([P, P], F32)
+                nc.vector.tensor_copy(out=gb_f[:], in_=gb_rows[:])
+                gb_ps = ps.tile([P, P], F32, tag="X")
+                nc.tensor.transpose(gb_ps[:], gb_f[:], ident[:])
+                nc.vector.tensor_copy(out=gb_col[:], in_=gb_ps[:, 0:16])
+                for h in range(2):
+                    cols = slice(D * h, D * (h + 1))
+                    nc.tensor.matmul(out=g2ps[:, cols], lhsT=ones[:], rhs=g2_rows[:, cols], start=True, stop=True)
+
+        steps = dict(
+            ld=load_z, zT=zT, zo=zo, zov=zov, zq=zq, mm1=mm1, B=Bi, Ge=Ge, Sq=Sq, st1=st1, N=N, Ng=Ng, T=T, A=A, Av=Av,
+            R=R, Rg=Rg, Q=Q, mm2=mm2, O1=O1, nm2=nm2, O2=O2, st2=st2, O3=O3, O4=O4, store=store,
+            w1p=w1p, w1q=w1q, w2p=w2p, w2q=w2q, gbs=gbs,
+        )
+        for b in range(-LAG, NB + LAG):
+            for name, off, i in PERIOD:
+                if 0 <= b + off < NB and not (name == "ld" and b + off < 3):
+                    steps[name](b + off, i)

@@ -160,13 +160,15 @@ def tile_emaaggregator_pa_t_kernel(tc, z, W1, b1, g1, be1, W2, b2, g2, be2, out)
         nc.vector.memset(g2_rows[:], 0.0)
         nc.scalar.dma_start(out=g2_rows[0:1, 0:D], in_=g2.rearrange("(o c) -> o c", o=1))
         nc.scalar.dma_start(out=g2_rows[0:1, D : 2 * D], in_=be2.rearrange("(o c) -> o c", o=1))
+        b_rows = const.tile([P, F + D], BF16)
+        nc.vector.memset(b_rows[:], 0.0)
+        nc.sync.dma_start(out=b_rows[0:1, 0:F], in_=b1.rearrange("(o c) -> o c", o=1))
+        nc.sync.dma_start(out=b_rows[0:1, F : F + D], in_=b2.rearrange("(o c) -> o c", o=1))
         b1b = const.tile([P, F], BF16)
-        nc.sync.dma_start(out=b1b[:], in_=b1.partition_broadcast(P))
         load_z(1, 0)
         w2r = hp.tile([P, 8, D], BF16, tag="hb")
         nc.sync.dma_start(out=w2r[:], in_=W2.rearrange("(ct p) n -> p ct n", p=P))
         b2b = const.tile([P, D], BF16)
-        nc.sync.dma_start(out=b2b[:], in_=b2.partition_broadcast(P))
         load_z(2, 0)
 
         ident = const.tile([P, P], F32)
@@ -426,6 +428,16 @@ def tile_emaaggregator_pa_t_kernel(tc, z, W1, b1, g1, be1, W2, b2, g2, be2, out)
                     cols = slice(D * h, D * (h + 1))
                     nc.tensor.matmul(out=g2ps[:, cols], lhsT=ones[:], rhs=g2_rows[:, cols], start=True, stop=True)
 
+        def spread_biases():
+            b1ps = ps.tile([P, F], BF16, tag="X")
+            for h in range(2):
+                cols = slice(512 * h, 512 * (h + 1))
+                nc.tensor.matmul(out=b1ps[:, cols], lhsT=ones[:], rhs=b_rows[:, cols], start=True, stop=True)
+            nc.scalar.copy(out=b1b[:], in_=b1ps[:])
+            b2ps = ps.tile([P, D], BF16, tag="X")
+            nc.tensor.matmul(out=b2ps[:], lhsT=ones[:], rhs=b_rows[:, F : F + D], start=True, stop=True)
+            nc.scalar.copy(out=b2b[:], in_=b2ps[:])
+
         steps = dict(
             ld=load_z, zT=zT, zo=zo, zov=zov, zq=zq, mm1=mm1, B=Bi, Ge=Ge, Sq=Sq, st1=st1, N=N, Ng=Ng, T=T, A=A, Av=Av,
             R=R, Rg=Rg, Q=Q, mm2=mm2, O1=O1, nm2=nm2, O2=O2, st2=st2, O3=O3, O4=O4, store=store,
@@ -435,3 +447,5 @@ def tile_emaaggregator_pa_t_kernel(tc, z, W1, b1, g1, be1, W2, b2, g2, be2, out)
             for name, off, i in PERIOD:
                 if 0 <= b + off < NB and not (name == "ld" and b + off < 3):
                     steps[name](b + off, i)
+                    if (name, b + off) == ("zo", 0):
+                        spread_biases()

@@ -19,6 +19,8 @@ BLK = NT * P
 NB = B // BLK
 FLOPS = 2 * B * D * F * 2
 EDGE = (0, NB - 1)
+AHEAD = (0, 1, 3)
+AFTER_AHEAD = 2
 LAG = 8
 
 PERIOD = (
@@ -282,11 +284,21 @@ def tile_emaaggregator_pa_t_kernel(tc, z, W1, b1, g1, be1, W2, b2, g2, be2, out)
         def Ng(b, j):
             norm_on(nc.vector if b in EDGE else nc.gpsimd, b, j)
 
+        def turn(b, ct, j):
+            nc.tensor.transpose(st[b]["ht", ct][:, P * j : P * (j + 1)], st[b]["n", j][:, P * ct : P * (ct + 1)], ident[:])
+
         def T(b, ct):
             ht = ps.tile([P, BLK], F32, tag="X")
-            for j in range(NT):
-                nc.tensor.transpose(ht[:, P * j : P * (j + 1)], st[b]["n", j][:, P * ct : P * (ct + 1)], ident[:])
             st[b]["ht", ct] = ht
+            if ct in AHEAD:
+                for j in range(NT - 1):
+                    turn(b, ct, j)
+                return
+            if ct == AFTER_AHEAD:
+                for c2 in AHEAD:
+                    turn(b, c2, NT - 1)
+            for j in range(NT):
+                turn(b, ct, j)
 
         def hb_of(b):
             if "hb" not in st[b]:

@@ -18,7 +18,6 @@ NT = 4
 BLK = NT * P
 NB = B // BLK
 FLOPS = 2 * B * D * F * 2
-EDGE = (0, NB - 1)
 AHEAD = (0, 1, 3)
 AFTER_AHEAD = 2
 LAG = 8
@@ -282,7 +281,8 @@ def tile_emaaggregator_pa_t_kernel(tc, z, W1, b1, g1, be1, W2, b2, g2, be2, out)
             norm_on(nc.vector, b, j)
 
         def Ng(b, j):
-            norm_on(nc.vector if b in EDGE else nc.gpsimd, b, j)
+            on_vector = b == 0 or (b == NB - 1 and j >= 2)
+            norm_on(nc.vector if on_vector else nc.gpsimd, b, j)
 
         def turn(b, ct, j):
             nc.tensor.transpose(st[b]["ht", ct][:, P * j : P * (j + 1)], st[b]["n", j][:, P * ct : P * (ct + 1)], ident[:])
@@ -328,7 +328,7 @@ def tile_emaaggregator_pa_t_kernel(tc, z, W1, b1, g1, be1, W2, b2, g2, be2, out)
             regroup(nc.vector, hg_of(b)[:, c], st[b]["hb"][:, 4 * c : 4 * c + 4, :])
 
         def Rg(b, c):
-            if b in EDGE:
+            if b == 0 or (b == NB - 1 and c == 1):
                 R(b, c)
                 return
             nc.gpsimd.tensor_scalar(

from contextlib import ExitStack

import concourse.mybir as mybir
from concourse.masks import make_identity

F32 = mybir.dt.float32
BF16 = mybir.dt.bfloat16
U32 = mybir.dt.uint32
U8 = mybir.dt.uint8
FP8X4 = mybir.dt.float8_e4m3fn_x4
ACT = mybir.ActivationFunctionType
ALU = mybir.AluOpType

P = 128
B, D, F = 4096, 512, 1024
EPS = 1e-5
NT = 4
BLK = NT * P
NB = B // BLK
FLOPS = 2 * B * D * F * 2
AHEAD = (0, 1, 3)
AFTER_AHEAD = 2
LAG = 8

PERIOD = (
    ("Rg", -2, 1),
    ("B", -1, 7),
    ("zo", 1, 0),
    ("Sq", -1, 1),
    ("Q", -2, 0),
    ("Q", -2, 1),
    ("st1", -1, 0),
    ("O3", -3, 3),
    ("w2q", -2, 1),
    ("mm1", 0, 1),
    ("B", 0, 0),
    ("O4", -3, 3),
    ("store", -3, 0),
    ("mm2", -2, 0),
    ("mm1", 0, 2),
    ("w2p", -1, 0),
    ("Ng", -1, 1),
    ("B", 0, 1),
    ("Ge", -1, 2),
    ("Ge", -1, 3),
    ("mm2", -2, 1),
    ("Ng", -1, 0),
    ("Sq", -1, 2),
    ("O1", -2, 0),
    ("B", 0, 2),
    ("mm2", -2, 2),
    ("Sq", -1, 3),
    ("mm1", 0, 3),
    ("O1", -2, 1),
    ("O1", -2, 2),
    ("gbs", -1, 0),
    ("B", 0, 3),
    ("st1", -1, 1),
    ("Ng", -1, 2),
    ("Ng", -1, 3),
    ("Ge", 0, 0),
    ("O2", -2, 0),
    ("w1p", 1, 0),
    ("Sq", 0, 0),
    ("mm2", -2, 3),
    ("O1", -2, 3),
    ("nm2", -2, 0),
    ("O3", -2, 0),
    ("O2", -2, 1),
    ("O2", -2, 2),
    ("zq", 1, 0),
    ("zT", 2, 1),
    ("w1p", 1, 1),
    ("st2", -2, 0),
    ("w2p", -1, 1),
    ("T", -1, 0),
    ("nm2", -2, 1),
    ("O2", -2, 3),
    ("O3", -2, 1),
    ("T", -1, 1),
    ("T", -1, 3),
    ("T", -1, 2),
    ("A", -1, 0),
    ("O3", -2, 2),
    ("T", -1, 4),
    ("st2", -2, 1),
    ("Av", -1, 3),
    ("A", -1, 1),
    ("T", -1, 6),
    ("A", -1, 2),
    ("O4", -2, 1),
    ("T", -1, 5),
    ("w2q", -1, 0),
    ("w1q", 1, 0),
    ("T", -1, 7),
    ("A", -1, 4),
    ("O4", -2, 0),
    ("Rg", -1, 0),
    ("mm1", 0, 4),
    ("Av", -1, 7),
    ("A", -1, 6),
    ("mm1", 0, 5),
    ("zT", 2, 0),
    ("ld", 3, 0),
    ("w1q", 1, 1),
    ("O4", -2, 2),
    ("A", -1, 5),
    ("B", 0, 4),
    ("mm1", 0, 6),
    ("mm1", 0, 7),
    ("zov", 2, 1),
    ("Ge", 0, 1),
    ("mm1", 1, 0),
    ("B", 0, 5),
    ("B", 0, 6),
)


def regroup(eng, dst, src):
    eng.tensor_copy(
        out=dst.rearrange("p (c i) t -> p c t i", i=4),
        in_=src.rearrange("p t (c i) -> p c t i", i=4),
    )


def tile_emaaggregator_pa_t_kernel(tc, z, W1, b1, g1, be1, W2, b2, g2, be2, out):
    nc = tc.nc
    with ExitStack() as ctx:
        const = ctx.enter_context(tc.tile_pool(name="const", bufs=1))
        zin = ctx.enter_context(tc.tile_pool(name="zin", bufs=4))
        zqp = ctx.enter_context(tc.tile_pool(name="zqp", bufs=3))
        xp = ctx.enter_context(tc.tile_pool(name="xp", bufs=4))
        gp = ctx.enter_context(tc.tile_pool(name="gp", bufs=12))
        jp = ctx.enter_context(tc.tile_pool(name="jp", bufs=2))
        hp = ctx.enter_context(tc.tile_pool(name="hp", bufs=2))
        op = ctx.enter_context(tc.tile_pool(name="op", bufs=6))
        ob = ctx.enter_context(tc.tile_pool(name="ob", bufs=2))
        sm = ctx.enter_context(tc.tile_pool(name="sm", bufs=3))
        ps = ctx.enter_context(tc.psum_pool(name="ps", bufs=4))
        ctx.enter_context(tc.manual_schedule())
        st = [dict() for b in range(NB)]

        def load_z(b, i):
            z_sb = zin.tile([P, NT * D], BF16, tag="z")
            nc.sync.dma_start(out=z_sb[:], in_=z[BLK * b : BLK * (b + 1), :].rearrange("(p j) k -> p (j k)", j=NT))
            st[b]["z"] = z_sb

        load_z(0, 0)
        w1r = hp.tile([P, 2, 4, 512], BF16, tag="hb")
        for h in range(2):
            for u in range(2):
                nc.sync.dma_start(
                    out=w1r[:, h, 2 * u : 2 * u + 2, :],
                    in_=W1[256 * u : 256 * (u + 1), 512 * h : 512 * (h + 1)].rearrange("(q e) c -> q e c", e=2),
                )
        gb_rows = const.tile([P, P], BF16)
        nc.vector.memset(gb_rows[:], 0.0)
        nc.scalar.dma_start(out=gb_rows[0:8, :], in_=g1.rearrange("(r c) -> r c", c=P))
        nc.scalar.dma_start(out=gb_rows[8:16, :], in_=be1.rearrange("(r c) -> r c", c=P))
        g2_rows = const.tile([P, 2 * D], BF16)
        nc.vector.memset(g2_rows[:], 0.0)
        nc.scalar.dma_start(out=g2_rows[0:1, 0:D], in_=g2.rearrange("(o c) -> o c", o=1))
        nc.scalar.dma_start(out=g2_rows[0:1, D : 2 * D], in_=be2.rearrange("(o c) -> o c", o=1))
        b_rows = const.tile([P, F + D], BF16)
        nc.vector.memset(b_rows[:], 0.0)
        nc.sync.dma_start(out=b_rows[0:1, 0:F], in_=b1.rearrange("(o c) -> o c", o=1))
        nc.sync.dma_start(out=b_rows[0:1, F : F + D], in_=b2.rearrange("(o c) -> o c", o=1))
        b1b = const.tile([P, F], BF16)
        load_z(1, 0)
        w2r = hp.tile([P, 8, D], BF16, tag="hb")
        nc.sync.dma_start(out=w2r[:], in_=W2.rearrange("(ct p) n -> p ct n", p=P))
        b2b = const.tile([P, D], BF16)
        load_z(2, 0)

        ident = const.tile([P, P], F32)
        make_identity(nc, ident[:])
        ones = const.tile([P, P], BF16)
        nc.vector.memset(ones[:], 1.0)
        neg_half = const.tile([P, 4], F32)
        nc.vector.memset(neg_half[:], -0.5)
        eps_t = const.tile([P, 1], F32)
        nc.vector.memset(eps_t[:], EPS)
        warm = const.tile([P, 1], F32)
        nc.scalar.activation(out=warm[:], in_=eps_t[:], func=ACT.Gelu)

        w1g = hp.tile([P, F, 4], BF16, tag="hg", align_bytes=64)
        w1c = const.tile([P, F], U32, align_bytes=64)
        w1s = const.tile([P, F], U8, align_bytes=64)
        w2g = hp.tile([P, 2, D, 4], BF16, tag="hg", align_bytes=64)
        w2c = const.tile([P, 2, D], U32, align_bytes=64)
        w2s = const.tile([P, 2, D], U8, align_bytes=64)
        gb_col = const.tile([P, 16], F32)
        g2ps = ps.tile([P, 2 * D], BF16, tag="C", bufs=1)

        def cols_of(b, keys):
            for key in keys:
                if key not in st[b]:
                    col = sm.tile([P, 4], F32, tag=key)
                    st[b][key] = col

        def zT(b, i):
            zw = st[b]["z"][:].bitcast(F32)
            zt = ps.tile([P, 2, 2, P], F32, tag="Y", bufs=3)
            for jj in range(2):
                for u in range(2):
                    c0 = (2 * i + jj) * 256 + u * P
                    nc.tensor.transpose(zt[:, jj, u, :], zw[:, c0 : c0 + P], ident[:])
            st[b]["zt", i] = zt

        def zo_on(copy, b, i):
            if "zg" not in st[b]:
                zg = zqp.tile([P, NT * P * 2], F32, tag="zg", align_bytes=64)
                st[b]["zg"] = zg
            zgv = st[b]["zg"][:].rearrange("q (j t u) -> q j t u", j=NT, u=2)
            copy(out=zgv[:, 2 * i : 2 * i + 2, :, :], in_=st[b]["zt", i][:].rearrange("q j u t -> q j t u"))

        def zo(b, i):
            zo_on(nc.scalar.copy, b, i)

        def zov(b, i):
            zo_on(nc.vector.tensor_copy, b, i)

        def zq(b, i):
            zc = zqp.tile([P, BLK], U32, tag="zc", align_bytes=64)
            zs = zqp.tile([P, BLK], U8, tag="zs", align_bytes=64)
            nc.vector.quantize_mx(out=zc[:].bitcast(FP8X4), scales=zs[:], in_=st[b]["zg"][:].bitcast(BF16))
            st[b]["zc"], st[b]["zs"] = zc, zs

        def mm1(b, i):
            j, h = i // 2, i % 2
            tok = slice(P * j, P * (j + 1))
            cols = slice(512 * h, 512 * (h + 1))
            acc = ps.tile([P, 512], F32, tag="X")
            nc.tensor.matmul_mx(
                out=acc[:],
                lhsT=st[b]["zc"][:, tok].bitcast(FP8X4),
                lhsT_scale=st[b]["zs"][:, tok],
                rhs=w1c[:, cols].bitcast(FP8X4),
                rhs_scale=w1s[:, cols],
                start=True,
                stop=True,
            )
            st[b]["acc", i] = acc

        def Bi(b, i):
            j, h = i // 2, i % 2
            cols = slice(512 * h, 512 * (h + 1))
            if h == 0:
                x = xp.tile([P, F], F32, tag="x")
                st[b]["x", j] = x
            nc.vector.tensor_tensor(out=st[b]["x", j][:, cols], in0=st[b]["acc", i][:], in1=b1b[:, cols], op=ALU.add)

        def Ge(b, j):
            cols_of(b, ("s1", "ss", "nm", "ve", "rs"))
            g = gp.tile([P, F], F32, tag="g")
            nc.scalar.activation(out=g[:], in_=st[b]["x", j][:], func=ACT.Gelu, accum_out=st[b]["s1"][:, j : j + 1])
            st[b]["g", j] = g

        def Sq(b, j):
            junk = jp.tile([P, F], BF16, tag="junk")
            nc.scalar.activation(
                out=junk[:], in_=st[b]["g", j][:], func=ACT.Square, scale=-float(F),
                bias=st[b]["s1"][:, j : j + 1], accum_out=st[b]["ss"][:, j : j + 1],
            )

        def rstd_cols(b, ss, ve, rs, cols, n):
            nc.scalar.activation(out=st[b][ve][:, cols], in_=st[b][ss][:, cols], func=ACT.Identity, scale=1.0 / (float(n) ** 3), bias=eps_t[:])
            nc.gpsimd.tensor_tensor(out=st[b][rs][:, cols], in0=st[b][ve][:, cols], in1=neg_half[:, cols], op=ALU.pow)

        def st1(b, i):
            cols = slice(2 * i, 2 * i + 2)
            nc.scalar.activation(out=st[b]["nm"][:, cols], in_=st[b]["s1"][:, cols], func=ACT.Identity, scale=-1.0 / F)
            rstd_cols(b, "ss", "ve", "rs", cols, F)

        def norm_on(eng, b, j):
            g = st[b]["g", j]
            eng.tensor_scalar(out=g[:], in0=g[:], scalar1=st[b]["nm"][:, j : j + 1], scalar2=st[b]["rs"][:, j : j + 1], op0=ALU.add, op1=ALU.mult)
            st[b]["n", j] = g

        def N(b, j):
            norm_on(nc.vector, b, j)

        def Ng(b, j):
            on_vector = b == 0 or (b == NB - 1 and j >= 2)
            norm_on(nc.vector if on_vector else nc.gpsimd, b, j)

        def turn(b, ct, j):
            nc.tensor.transpose(st[b]["ht", ct][:, P * j : P * (j + 1)], st[b]["n", j][:, P * ct : P * (ct + 1)], ident[:])

        def T(b, ct):
            ht = ps.tile([P, BLK], F32, tag="X")
            st[b]["ht", ct] = ht
            if ct in AHEAD:
                for j in range(NT - 1):
                    turn(b, ct, j)
                return
            if ct == AFTER_AHEAD:
                for c2 in AHEAD:
                    turn(b, c2, NT - 1)
            for j in range(NT):
                turn(b, ct, j)

        def hb_of(b):
            if "hb" not in st[b]:
                hb = hp.tile([P, 8, BLK], BF16, tag="hb")
                st[b]["hb"] = hb
            return st[b]["hb"]

        def A(b, ct):
            nc.scalar.activation(
                out=hb_of(b)[:, ct, :], in_=st[b]["ht", ct][:], func=ACT.Identity,
                scale=gb_col[:, ct : ct + 1], bias=gb_col[:, 8 + ct : 9 + ct],
            )

        def Av(b, ct):
            nc.vector.tensor_scalar(
                out=hb_of(b)[:, ct, :], in0=st[b]["ht", ct][:],
                scalar1=gb_col[:, ct : ct + 1], scalar2=gb_col[:, 8 + ct : 9 + ct], op0=ALU.mult, op1=ALU.add,
            )

        def hg_of(b):
            if "hg" not in st[b]:
                hg = hp.tile([P, 2, BLK, 4], BF16, tag="hg", align_bytes=64)
                st[b]["hg"] = hg
            return st[b]["hg"]

        def R(b, c):
            regroup(nc.vector, hg_of(b)[:, c], st[b]["hb"][:, 4 * c : 4 * c + 4, :])

        def Rg(b, c):
            if b == 0 or (b == NB - 1 and c == 1):
                R(b, c)
                return
            nc.gpsimd.tensor_scalar(
                out=hg_of(b)[:, c], in0=st[b]["hb"][:, 4 * c : 4 * c + 4, :].rearrange("p t w -> p w t"),
                scalar1=1.0, scalar2=0.0, op0=ALU.mult, op1=ALU.add,
            )

        def Q(b, c):
            if "hc" not in st[b]:
                hc = hp.tile([P, 2, BLK], U32, tag="hc", align_bytes=64)
                hs = hp.tile([P, 2, BLK], U8, tag="hs", align_bytes=64)
                st[b]["hc"], st[b]["hs"] = hc, hs
            nc.vector.quantize_mx(
                out=st[b]["hc"][:, c, :].bitcast(FP8X4),
                scales=st[b]["hs"][:, c, :],
                in_=st[b]["hg"][:, c].rearrange("p w t -> p (w t)"),
            )

        def mm2(b, j):
            tok = slice(P * j, P * (j + 1))
            y = ps.tile([P, D], F32, tag="Y", bufs=3)
            for c in range(2):
                nc.tensor.matmul_mx(
                    out=y[:],
                    lhsT=st[b]["hc"][:, c, tok].bitcast(FP8X4),
                    lhsT_scale=st[b]["hs"][:, c, tok],
                    rhs=w2c[:, c, :].bitcast(FP8X4),
                    rhs_scale=w2s[:, c, :],
                    start=(c == 0),
                    stop=(c == 1),
                )
            st[b]["y", j] = y

        def O1(b, j):
            cols_of(b, ("s2", "ss2", "nm2", "ve2", "rs2"))
            x2 = op.tile([P, D], F32, tag="x2")
            nc.vector.scalar_tensor_tensor(
                out=x2[:], in0=st[b]["y", j][:], scalar=1.0, in1=b2b[:], op0=ALU.mult, op1=ALU.add,
                accum_out=st[b]["s2"][:, j : j + 1],
            )
            st[b]["x2", j] = x2

        def nm2(b, i):
            cols = slice(2 * i, 2 * i + 2)
            nc.scalar.activation(out=st[b]["nm2"][:, cols], in_=st[b]["s2"][:, cols], func=ACT.Identity, scale=-1.0 / D)

        def O2(b, j):
            junk2 = jp.tile([P, D], BF16, tag="junk2")
            nc.scalar.activation(
                out=junk2[:], in_=st[b]["x2", j][:], func=ACT.Square, scale=-float(D),
                bias=st[b]["s2"][:, j : j + 1], accum_out=st[b]["ss2"][:, j : j + 1],
            )

        def st2(b, i):
            rstd_cols(b, "ss2", "ve2", "rs2", slice(2 * i, 2 * i + 2), D)

        def O3(b, j):
            t2 = op.tile([P, D], F32, tag="t2")
            nc.vector.scalar_tensor_tensor(
                out=t2[:], in0=st[b]["x2", j][:], scalar=st[b]["nm2"][:, j : j + 1], in1=g2ps[:, 0:D], op0=ALU.add, op1=ALU.mult
            )
            st[b]["t2", j] = t2

        def O4(b, j):
            if "o" not in st[b]:
                o = ob.tile([P, NT, D], F32, tag="o")
                st[b]["o"] = o
            nc.vector.scalar_tensor_tensor(
                out=st[b]["o"][:, j, :], in0=st[b]["t2", j][:], scalar=st[b]["rs2"][:, j : j + 1], in1=g2ps[:, D : 2 * D], op0=ALU.mult, op1=ALU.add
            )
            if b == NB - 1:
                nc.sync.dma_start(
                    out=out[BLK * b : BLK * (b + 1), :].rearrange("(p j) d -> p j d", j=NT)[:, j, :], in_=st[b]["o"][:, j, :]
                )

        def store(b, i):
            if b < NB - 1:
                nc.sync.dma_start(
                    out=out[BLK * b : BLK * (b + 1), :].rearrange("(p j) d -> p (j d)", j=NT),
                    in_=st[b]["o"][:].rearrange("p j d -> p (j d)"),
                )

        def w1p(b, h):
            if b == 0:
                cols = slice(512 * h, 512 * (h + 1))
                regroup(nc.vector, w1g[:, cols, :], w1r[:, h])

        def w1q(b, h):
            if b == 0:
                cols = slice(512 * h, 512 * (h + 1))
                nc.vector.quantize_mx(out=w1c[:, cols].bitcast(FP8X4), scales=w1s[:, cols], in_=w1g[:, cols, :].rearrange("p w t -> p (w t)"))

        def w2p(b, c):
            if b == 0:
                regroup(nc.vector, w2g[:, c], w2r[:, 4 * c : 4 * c + 4, :])

        def w2q(b, c):
            if b == 0:
                nc.vector.quantize_mx(out=w2c[:, c, :].bitcast(FP8X4), scales=w2s[:, c, :], in_=w2g[:, c].rearrange("p w t -> p (w t)"))

        def gbs(b, i):
            if b == 0:
                gb_f = const.tile([P, P], F32)
                nc.vector.tensor_copy(out=gb_f[:], in_=gb_rows[:])
                gb_ps = ps.tile([P, P], F32, tag="X")
                nc.tensor.transpose(gb_ps[:], gb_f[:], ident[:])
                nc.vector.tensor_copy(out=gb_col[:], in_=gb_ps[:, 0:16])
                for h in range(2):
                    cols = slice(D * h, D * (h + 1))
                    nc.tensor.matmul(out=g2ps[:, cols], lhsT=ones[:], rhs=g2_rows[:, cols], start=True, stop=True)

        def spread_biases():
            b1ps = ps.tile([P, F], BF16, tag="X")
            for h in range(2):
                cols = slice(512 * h, 512 * (h + 1))
                nc.tensor.matmul(out=b1ps[:, cols], lhsT=ones[:], rhs=b_rows[:, cols], start=True, stop=True)
            nc.scalar.copy(out=b1b[:], in_=b1ps[:])
            b2ps = ps.tile([P, D], BF16, tag="X")
            nc.tensor.matmul(out=b2ps[:], lhsT=ones[:], rhs=b_rows[:, F : F + D], start=True, stop=True)
            nc.scalar.copy(out=b2b[:], in_=b2ps[:])

        steps = dict(
            ld=load_z, zT=zT, zo=zo, zov=zov, zq=zq, mm1=mm1, B=Bi, Ge=Ge, Sq=Sq, st1=st1, N=N, Ng=Ng, T=T, A=A, Av=Av,
            R=R, Rg=Rg, Q=Q, mm2=mm2, O1=O1, nm2=nm2, O2=O2, st2=st2, O3=O3, O4=O4, store=store,
            w1p=w1p, w1q=w1q, w2p=w2p, w2q=w2q, gbs=gbs,
        )
        for b in range(-LAG, NB + LAG):
            for name, off, i in PERIOD:
                if 0 <= b + off < NB and not (name == "ld" and b + off < 3):
                    steps[name](b + off, i)
                    if (name, b + off) == ("zo", 0):
                        spread_biases()
